import numpy as np
import ml_dtypes


def mxq(x, axis, fmt="e4m3"):
    dtype, down = {"e4m3": (ml_dtypes.float8_e4m3fn, 7), "e5m2": (ml_dtypes.float8_e5m2, 14)}[fmt]
    v = np.moveaxis(np.asarray(x, np.float32).astype(ml_dtypes.bfloat16).astype(np.float64), axis, -1)
    blocks = v.reshape(v.shape[:-1] + (-1, 32))
    amax = np.abs(blocks).max(-1, keepdims=True)
    byte = np.maximum(np.where(amax > 0, np.frexp(amax)[1] - 1 + 127, 0) - down, 1)
    scale = np.exp2(byte - 127.0)
    codes = (blocks / scale).astype(np.float32).astype(dtype).astype(np.float64)
    return np.moveaxis((codes * scale).reshape(v.shape), -1, axis)


WIDE = False


def mx_kscale(k):
    if not WIDE:
        return np.ones(k)
    levels = np.array([10, -10, 5, -5, 0])
    a = np.random.permutation(np.resize(levels, k // 512 * 4)).reshape(k // 512, 4)
    idx = np.arange(k)
    return np.exp2(a[idx // 512, idx % 128 // 32])


BF16 = ml_dtypes.bfloat16


def bf(x):
    return np.asarray(x, np.float32).astype(BF16)


def f64(x):
    return np.asarray(x).astype(np.float64)


B, S, K, D, H, KV, HD = 8, 16, 32, 256, 8, 2, 128
T = S * K
REP = H // KV


def setup_inputs():
    t = mx_kscale(H * HD).reshape(KV, REP, HD)[:, 0, :]
    tw = np.repeat(t[:, None, :], REP, axis=1).reshape(H * HD)
    mu = 1.25 * np.sign(np.random.standard_normal((KV, HD)))
    return {"q_rot": bf(np.random.standard_normal((B, S, K, H, HD)) * 0.8),
            "k_rot": bf(np.random.standard_normal((B, S, K, KV, HD)) * 0.8),
            "v": bf((mu + np.random.standard_normal((B, S, K, KV, HD)) * 1.5) * t),
            "wo": bf(np.random.standard_normal((D, H * HD)) * 2.0 / np.sqrt(H * HD) / tw)}


def reference(q_rot, k_rot, v, wo):
    q = f64(q_rot).reshape(B, T, KV, REP, HD).transpose(0, 2, 3, 1, 4)
    kt = f64(k_rot).reshape(B, T, KV, 1, HD).transpose(0, 2, 3, 4, 1)
    vv = f64(v).reshape(B, T, KV, 1, HD).transpose(0, 2, 3, 1, 4)
    s = (q @ kt) * HD ** -0.5
    e = np.exp(s - s.max(-1, keepdims=True))
    o = (mxq(e, 4, "e4m3") @ mxq(vv, 3, "e4m3")) / e.sum(-1, keepdims=True)
    o = o.transpose(0, 3, 1, 2, 4).reshape(B, T, H * HD)
    return (mxq(o, 2, "e4m3") @ mxq(f64(wo), 1, "e4m3").T).reshape(B, S, K, D)

@@ -1,0 +1,369 @@
+from contextlib import ExitStack
+
+import concourse.mybir as mybir
+from concourse.masks import make_identity
+
+F32 = mybir.dt.float32
+BF16 = mybir.dt.bfloat16
+U32 = mybir.dt.uint32
+U8 = mybir.dt.uint8
+FP8X4 = mybir.dt.float8_e4m3fn_x4
+EXP = mybir.ActivationFunctionType.Exp
+ALONG_ROW = mybir.AxisListType.X
+MULT = mybir.AluOpType.mult
+
+P = 128
+PACK = 4
+BATCH = 8
+POSITIONS = 512
+TILES = POSITIONS // P
+GROUPS = 2
+REP = 4
+HEADS = GROUPS * REP
+HEAD_DIM = 128
+FEATURES = HEADS * HEAD_DIM
+MODEL = 256
+SCALE = HEAD_DIM ** -0.5
+UNITS_PER_TILE = 4
+E_ON_VECTOR_EVERY = 4
+
+FLOPS = 2 * BATCH * HEADS * POSITIONS * POSITIONS * HEAD_DIM * 2 + 2 * BATCH * POSITIONS * FEATURES * MODEL
+
+
+def tile_attention_pb_t_kernel(tc, q_rot, k_rot, v, wo, out):
+    nc = tc.nc
+    n_tiles = BATCH * TILES
+    n_units = n_tiles * UNITS_PER_TILE
+    with ExitStack() as ctx:
+        ctx.enter_context(tc.manual_schedule())
+        constants = ctx.enter_context(tc.tile_pool(name="constants", bufs=1))
+        resident = ctx.enter_context(tc.tile_pool(name="resident", bufs=1))
+        per_batch = ctx.enter_context(tc.tile_pool(name="per_batch", bufs=2))
+        per_tile = ctx.enter_context(tc.tile_pool(name="per_tile", bufs=3))
+        per_unit = ctx.enter_context(tc.tile_pool(name="per_unit", bufs=5))
+        results = ctx.enter_context(tc.tile_pool(name="results", bufs=8))
+        score_banks = ctx.enter_context(tc.psum_pool(name="score_banks", bufs=4))
+        eT_banks = ctx.enter_context(tc.psum_pool(name="eT_banks", bufs=2))
+        o_bank = ctx.enter_context(tc.psum_pool(name="o_bank", bufs=1))
+        side_bank = ctx.enter_context(tc.psum_pool(name="side_bank", bufs=1))
+
+        k_sb, q_sb, v_sb = [], [], []
+        for b in range(BATCH):
+            keys = resident.tile([P, TILES, GROUPS * HEAD_DIM], BF16, name="keys%d" % b)
+            queries = resident.tile([P, TILES, FEATURES], BF16, name="queries%d" % b)
+            values = resident.tile([P, PACK, GROUPS * HEAD_DIM], BF16, name="values%d" % b)
+            k_sb.append(keys)
+            q_sb.append(queries)
+            v_sb.append(values)
+        wo_sb = resident.tile([P, 2 * FEATURES], BF16)
+
+        def load_keys(b):
+            nc.sync.dma_start(
+                out=k_sb[b][:],
+                in_=k_rot[b].rearrange("s k g d -> (s k) (g d)").rearrange("(t p) f -> p t f", p=P),
+            )
+
+        def load_queries(b, j):
+            nc.sync.dma_start(
+                out=q_sb[b][:, j, :],
+                in_=q_rot[b].rearrange("s k h d -> (s k) (h d)").rearrange("(p j) f -> p j f", j=TILES)[:, j, :],
+            )
+
+        def load_values(b):
+            nc.sync.dma_start(
+                out=v_sb[b][:].rearrange("p (u e) c -> p u (e c)", u=2),
+                in_=v[b].rearrange("s k g d -> (s k) (g d)").rearrange("(u p e) c -> p u (e c)", u=2, e=2),
+            )
+
+        load_keys(0)
+        load_queries(0, 0)
+        nc.sync.dma_start(
+            out=wo_sb[:].rearrange("p (a f) -> p a f", a=2), in_=wo.rearrange("(a p) f -> p a f", p=P)
+        )
+        load_values(0)
+        for j in range(1, TILES):
+            load_queries(0, j)
+        for b in range(1, BATCH):
+            load_keys(b)
+            for j in range(TILES):
+                load_queries(b, j)
+            load_values(b)
+        out_rows = [
+            out[b].rearrange("s k m -> (s k) m").rearrange("(p j) m -> p j m", j=TILES) for b in range(BATCH)
+        ]
+
+        identity_bf16 = constants.tile([P, P], BF16)
+        make_identity(nc, identity_bf16[:])
+        identity_f32 = constants.tile([P, P], F32)
+        make_identity(nc, identity_f32[:])
+
+        zero = constants.tile([P, 1], F32)
+        nc.vector.memset(zero[:], 0.0)
+        one = constants.tile([P, 1], F32)
+        nc.scalar.activation(out=one[:], in_=zero[:], func=EXP)
+
+        kT_of, v_codes_of, v_scales_of = {}, {}, {}
+        qT_of, o_sb_of, o_grouped_of, o_codes_of, o_scales_of = {}, {}, {}, {}, {}
+        row_sum_of, inv_sum_of, o_ps_of = {}, {}, {}
+        row_max_of, neg_max_of, scores_of, e_sb_of, eT_of, e_grouped_of, e_codes_of, e_scales_of = (
+            {}, {}, {}, {}, {}, {}, {}, {},
+        )
+
+        def transpose_keys(b):
+            kT_ps = side_bank.tile([P, GROUPS, TILES, P], BF16, tag="side")
+            for g in range(GROUPS):
+                for t in range(TILES):
+                    nc.tensor.transpose(
+                        kT_ps[:, g, t, :], k_sb[b][:, t, g * HEAD_DIM : (g + 1) * HEAD_DIM], identity_bf16[:]
+                    )
+            return kT_ps
+
+        def keep_keys(b, kT_ps):
+            kT = per_batch.tile([P, GROUPS, POSITIONS], BF16)
+            nc.scalar.copy(out=kT[:], in_=kT_ps[:].rearrange("d g t k -> d g (t k)"))
+            kT_of[b] = kT
+
+        def transpose_queries(t):
+            qT_ps = side_bank.tile([P, HEADS, P], BF16, tag="side")
+            for h in range(HEADS):
+                nc.tensor.transpose(
+                    qT_ps[:, h, :],
+                    q_sb[t // TILES][:, t % TILES, h * HEAD_DIM : (h + 1) * HEAD_DIM],
+                    identity_bf16[:],
+                )
+            return qT_ps
+
+        def keep_queries(t, qT_ps):
+            qT = per_tile.tile([P, HEADS, P], BF16)
+            nc.scalar.copy(out=qT[:], in_=qT_ps[:])
+            qT_of[t] = qT
+
+        def quantise_values(b):
+            v_grouped = per_batch.tile([P, GROUPS * HEAD_DIM, PACK], BF16, align_bytes=64)
+            nc.vector.tensor_copy(out=v_grouped[:], in_=v_sb[b][:].rearrange("p t c -> p c t"))
+            v_codes = per_batch.tile([P, GROUPS * HEAD_DIM], U32, align_bytes=64)
+            v_scales = per_batch.tile([P, GROUPS * HEAD_DIM], U8, align_bytes=64)
+            nc.vector.quantize_mx(
+                out=v_codes[:].bitcast(FP8X4),
+                scales=v_scales[:],
+                in_=v_grouped[:].rearrange("p c t -> p (c t)"),
+            )
+            v_codes_of[b] = v_codes
+            v_scales_of[b] = v_scales
+
+        def score_tile(n, a):
+            t = n // UNITS_PER_TILE
+            head = (n % UNITS_PER_TILE) * 2 + a
+            if a == 0:
+                row_max = per_unit.tile([P, 2], F32)
+                row_max_of[n] = row_max
+            s_ps = score_banks.tile([P, POSITIONS], F32)
+            nc.tensor.matmul(
+                out=s_ps[:], lhsT=qT_of[t][:, head, :], rhs=kT_of[t // TILES][:, head // REP, :], start=True, stop=True
+            )
+            nc.vector.reduce_max(out=row_max_of[n][:, a : a + 1], in_=s_ps[:], axis=ALONG_ROW)
+            scores_of[n, a] = s_ps
+
+        def negate_maxima(n):
+            neg_max = per_unit.tile([P, 2], F32)
+            nc.gpsimd.tensor_scalar_mul(out=neg_max[:], in0=row_max_of[n][:], scalar1=-SCALE)
+            neg_max_of[n] = neg_max
+
+        def exponential(n, a):
+            if a == 0:
+                e_sb = per_unit.tile([P, 2 * POSITIONS], BF16)
+                e_sb_of[n] = e_sb
+                eT_ps = eT_banks.tile([P, 2, 2, P], F32)
+                eT_of[n] = eT_ps
+                if n % 2 == 0:
+                    row_sum = per_unit.tile([P, REP], F32)
+                    row_sum_of[n // 2] = row_sum
+            i = 2 * (n % 2) + a
+            nc.scalar.activation(
+                out=e_sb_of[n][:, a * POSITIONS : (a + 1) * POSITIONS],
+                in_=scores_of[n, a][:],
+                func=EXP,
+                bias=neg_max_of[n][:, a : a + 1],
+                scale=SCALE,
+                accum_out=row_sum_of[n // 2][:, i : i + 1],
+            )
+            e_words = e_sb_of[n][:].bitcast(F32)
+            for u in range(2):
+                first = (2 * a + u) * P
+                nc.tensor.transpose(eT_of[n][:, a, u, :], e_words[:, first : first + P], identity_f32[:])
+
+        def leaves_on_vector(n):
+            return n % E_ON_VECTOR_EVERY == E_ON_VECTOR_EVERY - 1
+
+        def group_e(n):
+            e_grouped = per_unit.tile([P, 2 * P * PACK], BF16, align_bytes=64)
+            grouped_words = e_grouped[:].bitcast(F32).rearrange("p (a q u) -> p a q u", a=2, u=2)
+            if leaves_on_vector(n):
+                nc.vector.tensor_copy(out=grouped_words, in_=eT_of[n][:].rearrange("p a u q -> p a q u"))
+            else:
+                nc.scalar.copy(out=grouped_words, in_=eT_of[n][:].rearrange("p a u q -> p a q u"))
+            e_grouped_of[n] = e_grouped
+
+        def quantise_e(n):
+            e_codes = per_unit.tile([P, 2 * P], U32, align_bytes=64)
+            e_scales = per_unit.tile([P, 2 * P], U8, align_bytes=64)
+            nc.vector.quantize_mx(out=e_codes[:].bitcast(FP8X4), scales=e_scales[:], in_=e_grouped_of[n][:])
+            e_codes_of[n] = e_codes
+            e_scales_of[n] = e_scales
+
+        def invert_sums(r):
+            inv_sum = per_unit.tile([P, REP], F32)
+            nc.vector.reciprocal(out=inv_sum[:], in_=row_sum_of[r][:])
+            inv_sum_of[r] = inv_sum
+
+        def multiply_by_v(r):
+            b = r // (TILES * GROUPS)
+            g_cols = slice((r % GROUPS) * HEAD_DIM, (r % GROUPS + 1) * HEAD_DIM)
+            o_ps = o_bank.tile([P, REP, HEAD_DIM], F32)
+            for i in range(REP):
+                n = 2 * r + i // 2
+                q_cols = slice((i % 2) * P, (i % 2 + 1) * P)
+                nc.tensor.matmul_mx(
+                    out=o_ps[:, i, :],
+                    lhsT=e_codes_of[n][:, q_cols].bitcast(FP8X4),
+                    lhsT_scale=e_scales_of[n][:, q_cols],
+                    rhs=v_codes_of[b][:, g_cols].bitcast(FP8X4),
+                    rhs_scale=v_scales_of[b][:, g_cols],
+                    start=True,
+                    stop=True,
+                )
+            o_ps_of[r] = o_ps
+
+        def normalise(r):
+            t = r // GROUPS
+            g = r % GROUPS
+            if g == 0:
+                o_sb = per_tile.tile([P, FEATURES], BF16)
+                o_sb_of[t] = o_sb
+            nc.vector.tensor_tensor(
+                out=o_sb_of[t][:, g * REP * HEAD_DIM : (g + 1) * REP * HEAD_DIM].rearrange("p (i d) -> p i d", i=REP),
+                in0=o_ps_of[r][:],
+                in1=inv_sum_of[r][:].unsqueeze(2).to_broadcast([P, REP, HEAD_DIM]),
+                op=MULT,
+            )
+
+        def transpose_o(t):
+            o_words = o_sb_of[t][:].bitcast(F32)
+            oT_ps = side_bank.tile([P, GROUPS, 2, P], F32, tag="side")
+            for g in range(GROUPS):
+                for u in range(2):
+                    first = (2 * g + u) * P
+                    nc.tensor.transpose(oT_ps[:, g, u, :], o_words[:, first : first + P], identity_f32[:])
+            return oT_ps
+
+        def group_o(t, oT_ps):
+            o_grouped = per_tile.tile([P, GROUPS * P * PACK], BF16, align_bytes=64)
+            nc.scalar.copy(
+                out=o_grouped[:].bitcast(F32).rearrange("p (g q u) -> p g q u", g=GROUPS, u=2),
+                in_=oT_ps[:].rearrange("p g u q -> p g q u"),
+            )
+            o_grouped_of[t] = o_grouped
+
+        def quantise_o(t):
+            o_codes = per_tile.tile([P, GROUPS * P], U32, align_bytes=64)
+            o_scales = per_tile.tile([P, GROUPS * P], U8, align_bytes=64)
+            nc.vector.quantize_mx(out=o_codes[:].bitcast(FP8X4), scales=o_scales[:], in_=o_grouped_of[t][:])
+            o_codes_of[t] = o_codes
+            o_scales_of[t] = o_scales
+
+        def project(t):
+            out_ps = side_bank.tile([P, MODEL], F32, tag="side")
+            for g in range(GROUPS):
+                nc.tensor.matmul_mx(
+                    out=out_ps[:],
+                    lhsT=o_codes_of[t][:, g * P : (g + 1) * P].bitcast(FP8X4),
+                    lhsT_scale=o_scales_of[t][:, g * P : (g + 1) * P],
+                    rhs=wo_codes[:, g * MODEL : (g + 1) * MODEL].bitcast(FP8X4),
+                    rhs_scale=wo_scales[:, g * MODEL : (g + 1) * MODEL],
+                    start=(g == 0),
+                    stop=(g == GROUPS - 1),
+                )
+            return out_ps
+
+        def store(t, out_ps):
+            out_sb = results.tile([P, MODEL], F32)
+            nc.scalar.copy(out=out_sb[:], in_=out_ps[:])
+            nc.sync.dma_start(out=out_rows[t // TILES][:, t % TILES, :], in_=out_sb[:])
+
+        keep_keys(0, transpose_keys(0))
+        keep_queries(0, transpose_queries(0))
+        for n in range(2):
+            for a in range(2):
+                score_tile(n, a)
+            negate_maxima(n)
+
+        wo_words = wo_sb[:].bitcast(F32)
+        wo_grouped = constants.tile([P, GROUPS * MODEL * PACK], BF16, align_bytes=64)
+        wo_codes = constants.tile([P, GROUPS * MODEL], U32, align_bytes=64)
+        wo_scales = constants.tile([P, GROUPS * MODEL], U8, align_bytes=64)
+        for g in range(GROUPS):
+            eT_ps = eT_banks.tile([P, 2, 2, P], F32)
+            for u in range(2):
+                for a in range(2):
+                    first = a * (FEATURES // 2) + (2 * g + u) * P
+                    nc.tensor.transpose(eT_ps[:, u, a, :], wo_words[:, first : first + P], identity_f32[:])
+            nc.vector.tensor_copy(
+                out=wo_grouped[:].bitcast(F32)[:, g * 2 * MODEL : (g + 1) * 2 * MODEL].rearrange(
+                    "p (m u) -> p m u", u=2
+                ),
+                in_=eT_ps[:].rearrange("p u a m -> p (a m) u"),
+            )
+        quantise_values(0)
+        nc.vector.quantize_mx(out=wo_codes[:].bitcast(FP8X4), scales=wo_scales[:], in_=wo_grouped[:])
+
+        side_ps = None
+        for n in range(n_units + 8):
+            phase = n % UNITS_PER_TILE
+            t = n // UNITS_PER_TILE
+            r = (n - 2) // 2
+            round_ready = n % 2 == 1 and 0 <= r < n_tiles * GROUPS
+            new_batch = (t + 2) % TILES == 0 and t + 2 < n_tiles
+
+            if 1 <= n <= n_units and leaves_on_vector(n - 1):
+                group_e(n - 1)
+
+            for a in range(2):
+                if n < n_units:
+                    exponential(n, a)
+                if n + 2 < n_units:
+                    score_tile(n + 2, a)
+            if n + 2 < n_units:
+                negate_maxima(n + 2)
+            if round_ready:
+                invert_sums(r)
+
+            if 1 <= n <= n_units and not leaves_on_vector(n - 1):
+                group_e(n - 1)
+            if phase == 0 and 0 <= t - 2 < n_tiles:
+                group_o(t - 2, side_ps)
+            if phase == 1 and t + 1 < n_tiles:
+                keep_queries(t + 1, side_ps)
+            if phase == 2 and 0 <= t - 2 < n_tiles:
+                store(t - 2, side_ps)
+            if phase == 3 and new_batch:
+                keep_keys((t + 2) // TILES, side_ps)
+
+            if round_ready:
+                multiply_by_v(r)
+            if 1 <= n <= n_units:
+                quantise_e(n - 1)
+            if phase == 0 and 0 <= t - 2 < n_tiles:
+                quantise_o(t - 2)
+            if phase == 2 and new_batch:
+                quantise_values((t + 2) // TILES)
+            if round_ready:
+                normalise(r)
+
+            if phase == 0 and t + 1 < n_tiles:
+                side_ps = transpose_queries(t + 1)
+            if phase == 1 and 0 <= t - 2 < n_tiles:
+                side_ps = project(t - 2)
+            if phase == 2 and new_batch:
+                side_ps = transpose_keys((t + 2) // TILES)
+            if phase == 3 and 0 <= t - 1 < n_tiles:
+                side_ps = transpose_o(t - 1)

@@ -25,7 +25,7 @@ FEATURES = HEADS * HEAD_DIM
 MODEL = 256
 SCALE = HEAD_DIM ** -0.5
 UNITS_PER_TILE = 4
-E_ON_VECTOR_EVERY = 4
+E_ON_VECTOR_EVERY = 2
 
 FLOPS = 2 * BATCH * HEADS * POSITIONS * POSITIONS * HEAD_DIM * 2 + 2 * BATCH * POSITIONS * FEATURES * MODEL
 

@@ -25,7 +25,7 @@ FEATURES = HEADS * HEAD_DIM
 MODEL = 256
 SCALE = HEAD_DIM ** -0.5
 UNITS_PER_TILE = 4
-E_ON_VECTOR_EVERY = 2
+E_ON_VECTOR_EVERY = 4
 
 FLOPS = 2 * BATCH * HEADS * POSITIONS * POSITIONS * HEAD_DIM * 2 + 2 * BATCH * POSITIONS * FEATURES * MODEL
 
@@ -77,10 +77,10 @@ def tile_attention_pb_t_kernel(tc, q_rot, k_rot, v, wo, out):
 
         load_keys(0)
         load_queries(0, 0)
+        load_values(0)
         nc.sync.dma_start(
             out=wo_sb[:].rearrange("p (a f) -> p a f", a=2), in_=wo.rearrange("(a p) f -> p a f", p=P)
         )
-        load_values(0)
         for j in range(1, TILES):
             load_queries(0, j)
         for b in range(1, BATCH):
@@ -120,7 +120,10 @@ def tile_attention_pb_t_kernel(tc, q_rot, k_rot, v, wo, out):
 
         def keep_keys(b, kT_ps):
             kT = per_batch.tile([P, GROUPS, POSITIONS], BF16)
-            nc.scalar.copy(out=kT[:], in_=kT_ps[:].rearrange("d g t k -> d g (t k)"))
+            nc.scalar.copy(
+                out=kT[:].rearrange("d g k -> d (g k)").bitcast(F32),
+                in_=kT_ps[:].rearrange("d g t k -> d (g t k)").bitcast(F32),
+            )
             kT_of[b] = kT
 
         def transpose_queries(t):
@@ -135,7 +138,10 @@ def tile_attention_pb_t_kernel(tc, q_rot, k_rot, v, wo, out):
 
         def keep_queries(t, qT_ps):
             qT = per_tile.tile([P, HEADS, P], BF16)
-            nc.scalar.copy(out=qT[:], in_=qT_ps[:])
+            nc.scalar.copy(
+                out=qT[:].rearrange("d h q -> d (h q)").bitcast(F32),
+                in_=qT_ps[:].rearrange("d h q -> d (h q)").bitcast(F32),
+            )
             qT_of[t] = qT
 
         def quantise_values(b):
@@ -196,20 +202,22 @@ def tile_attention_pb_t_kernel(tc, q_rot, k_rot, v, wo, out):
             return n % E_ON_VECTOR_EVERY == E_ON_VECTOR_EVERY - 1
 
         def group_e(n):
-            e_grouped = per_unit.tile([P, 2 * P * PACK], BF16, align_bytes=64)
-            grouped_words = e_grouped[:].bitcast(F32).rearrange("p (a q u) -> p a q u", a=2, u=2)
+            if n % 2 == 0:
+                e_grouped = per_unit.tile([P, REP * P * PACK], BF16, align_bytes=64)
+                e_grouped_of[n // 2] = e_grouped
+            half = slice((n % 2) * POSITIONS, (n % 2 + 1) * POSITIONS)
+            grouped_words = e_grouped_of[n // 2][:].bitcast(F32)[:, half].rearrange("p (a q u) -> p a q u", a=2, u=2)
             if leaves_on_vector(n):
                 nc.vector.tensor_copy(out=grouped_words, in_=eT_of[n][:].rearrange("p a u q -> p a q u"))
             else:
                 nc.scalar.copy(out=grouped_words, in_=eT_of[n][:].rearrange("p a u q -> p a q u"))
-            e_grouped_of[n] = e_grouped
 
-        def quantise_e(n):
-            e_codes = per_unit.tile([P, 2 * P], U32, align_bytes=64)
-            e_scales = per_unit.tile([P, 2 * P], U8, align_bytes=64)
-            nc.vector.quantize_mx(out=e_codes[:].bitcast(FP8X4), scales=e_scales[:], in_=e_grouped_of[n][:])
-            e_codes_of[n] = e_codes
-            e_scales_of[n] = e_scales
+        def quantise_e(r):
+            e_codes = per_unit.tile([P, REP * P], U32, align_bytes=64)
+            e_scales = per_unit.tile([P, REP * P], U8, align_bytes=64)
+            nc.vector.quantize_mx(out=e_codes[:].bitcast(FP8X4), scales=e_scales[:], in_=e_grouped_of[r][:])
+            e_codes_of[r] = e_codes
+            e_scales_of[r] = e_scales
 
         def invert_sums(r):
             inv_sum = per_unit.tile([P, REP], F32)
@@ -221,12 +229,11 @@ def tile_attention_pb_t_kernel(tc, q_rot, k_rot, v, wo, out):
             g_cols = slice((r % GROUPS) * HEAD_DIM, (r % GROUPS + 1) * HEAD_DIM)
             o_ps = o_bank.tile([P, REP, HEAD_DIM], F32)
             for i in range(REP):
-                n = 2 * r + i // 2
-                q_cols = slice((i % 2) * P, (i % 2 + 1) * P)
+                q_cols = slice(i * P, (i + 1) * P)
                 nc.tensor.matmul_mx(
                     out=o_ps[:, i, :],
-                    lhsT=e_codes_of[n][:, q_cols].bitcast(FP8X4),
-                    lhsT_scale=e_scales_of[n][:, q_cols],
+                    lhsT=e_codes_of[r][:, q_cols].bitcast(FP8X4),
+                    lhsT_scale=e_scales_of[r][:, q_cols],
                     rhs=v_codes_of[b][:, g_cols].bitcast(FP8X4),
                     rhs_scale=v_scales_of[b][:, g_cols],
                     start=True,
@@ -287,11 +294,12 @@ def tile_attention_pb_t_kernel(tc, q_rot, k_rot, v, wo, out):
 
         def store(t, out_ps):
             out_sb = results.tile([P, MODEL], F32)
-            nc.scalar.copy(out=out_sb[:], in_=out_ps[:])
+            nc.vector.tensor_copy(out=out_sb[:], in_=out_ps[:])
             nc.sync.dma_start(out=out_rows[t // TILES][:, t % TILES, :], in_=out_sb[:])
 
         keep_keys(0, transpose_keys(0))
         keep_queries(0, transpose_queries(0))
+        quantise_values(0)
         for n in range(2):
             for a in range(2):
                 score_tile(n, a)
@@ -313,7 +321,6 @@ def tile_attention_pb_t_kernel(tc, q_rot, k_rot, v, wo, out):
                 ),
                 in_=eT_ps[:].rearrange("p u a m -> p (a m) u"),
             )
-        quantise_values(0)
         nc.vector.quantize_mx(out=wo_codes[:].bitcast(FP8X4), scales=wo_scales[:], in_=wo_grouped[:])
 
         side_ps = None
@@ -326,6 +333,8 @@ def tile_attention_pb_t_kernel(tc, q_rot, k_rot, v, wo, out):
 
             if 1 <= n <= n_units and leaves_on_vector(n - 1):
                 group_e(n - 1)
+            if phase == 2 and 0 <= t - 2 < n_tiles:
+                store(t - 2, side_ps)
 
             for a in range(2):
                 if n < n_units:
@@ -334,8 +343,6 @@ def tile_attention_pb_t_kernel(tc, q_rot, k_rot, v, wo, out):
                     score_tile(n + 2, a)
             if n + 2 < n_units:
                 negate_maxima(n + 2)
-            if round_ready:
-                invert_sums(r)
 
             if 1 <= n <= n_units and not leaves_on_vector(n - 1):
                 group_e(n - 1)
@@ -343,15 +350,14 @@ def tile_attention_pb_t_kernel(tc, q_rot, k_rot, v, wo, out):
                 group_o(t - 2, side_ps)
             if phase == 1 and t + 1 < n_tiles:
                 keep_queries(t + 1, side_ps)
-            if phase == 2 and 0 <= t - 2 < n_tiles:
-                store(t - 2, side_ps)
             if phase == 3 and new_batch:
                 keep_keys((t + 2) // TILES, side_ps)
 
             if round_ready:
                 multiply_by_v(r)
-            if 1 <= n <= n_units:
-                quantise_e(n - 1)
+            if n % 2 == 0 and 2 <= n <= n_units:
+                quantise_e((n - 2) // 2)
+                invert_sums((n - 2) // 2)
             if phase == 0 and 0 <= t - 2 < n_tiles:
                 quantise_o(t - 2)
             if phase == 2 and new_batch:

@@ -25,7 +25,7 @@ FEATURES = HEADS * HEAD_DIM
 MODEL = 256
 SCALE = HEAD_DIM ** -0.5
 UNITS_PER_TILE = 4
-E_ON_VECTOR_EVERY = 4
+PARK_ROWS = P * HEADS // MODEL
 
 FLOPS = 2 * BATCH * HEADS * POSITIONS * POSITIONS * HEAD_DIM * 2 + 2 * BATCH * POSITIONS * FEATURES * MODEL
 
@@ -66,7 +66,7 @@ def tile_attention_pb_t_kernel(tc, q_rot, k_rot, v, wo, out):
         def load_queries(b, j):
             nc.sync.dma_start(
                 out=q_sb[b][:, j, :],
-                in_=q_rot[b].rearrange("s k h d -> (s k) (h d)").rearrange("(p j) f -> p j f", j=TILES)[:, j, :],
+                in_=q_rot[b].rearrange("s k h d -> (s k) (h d)")[j * P : (j + 1) * P, :],
             )
 
         def load_values(b):
@@ -83,14 +83,11 @@ def tile_attention_pb_t_kernel(tc, q_rot, k_rot, v, wo, out):
         )
         for j in range(1, TILES):
             load_queries(0, j)
-        for b in range(1, BATCH):
-            load_keys(b)
-            for j in range(TILES):
-                load_queries(b, j)
-            load_values(b)
-        out_rows = [
-            out[b].rearrange("s k m -> (s k) m").rearrange("(p j) m -> p j m", j=TILES) for b in range(BATCH)
-        ]
+        out_flat = [out[b].rearrange("s k m -> (s k) m") for b in range(BATCH)]
+
+        def out_rows(t, count):
+            first = (t % TILES) * P
+            return out_flat[t // TILES][first : first + count, :]
 
         identity_bf16 = constants.tile([P, P], BF16)
         make_identity(nc, identity_bf16[:])
@@ -103,46 +100,46 @@ def tile_attention_pb_t_kernel(tc, q_rot, k_rot, v, wo, out):
         nc.scalar.activation(out=one[:], in_=zero[:], func=EXP)
 
         kT_of, v_codes_of, v_scales_of = {}, {}, {}
-        qT_of, o_sb_of, o_grouped_of, o_codes_of, o_scales_of = {}, {}, {}, {}, {}
-        row_sum_of, inv_sum_of, o_ps_of = {}, {}, {}
+        qT_of, o_grouped_of, o_codes_of, o_scales_of = {}, {}, {}, {}
+        row_sum_of, factors_of, o_ps_of = {}, {}, {}
         row_max_of, neg_max_of, scores_of, e_sb_of, eT_of, e_grouped_of, e_codes_of, e_scales_of = (
             {}, {}, {}, {}, {}, {}, {}, {},
         )
 
-        def transpose_keys(b):
-            kT_ps = side_bank.tile([P, GROUPS, TILES, P], BF16, tag="side")
-            for g in range(GROUPS):
+        def transpose_keys(b, kT_ps, groups):
+            for g in groups:
                 for t in range(TILES):
                     nc.tensor.transpose(
                         kT_ps[:, g, t, :], k_sb[b][:, t, g * HEAD_DIM : (g + 1) * HEAD_DIM], identity_bf16[:]
                     )
-            return kT_ps
 
-        def keep_keys(b, kT_ps):
-            kT = per_batch.tile([P, GROUPS, POSITIONS], BF16)
-            nc.scalar.copy(
-                out=kT[:].rearrange("d g k -> d (g k)").bitcast(F32),
-                in_=kT_ps[:].rearrange("d g t k -> d (g t k)").bitcast(F32),
+        def keep_keys(b, kT_ps, groups, copy):
+            if b not in kT_of:
+                kT = per_batch.tile([P, GROUPS, POSITIONS], BF16)
+                kT_of[b] = kT
+            some = slice(groups.start, groups.stop)
+            copy(
+                out=kT_of[b][:, some, :].rearrange("d g k -> d (g k)").bitcast(F32),
+                in_=kT_ps[:, some, :, :].rearrange("d g t k -> d (g t k)").bitcast(F32),
             )
-            kT_of[b] = kT
 
-        def transpose_queries(t):
-            qT_ps = side_bank.tile([P, HEADS, P], BF16, tag="side")
-            for h in range(HEADS):
+        def transpose_queries(t, qT_ps, heads):
+            for h in heads:
                 nc.tensor.transpose(
                     qT_ps[:, h, :],
                     q_sb[t // TILES][:, t % TILES, h * HEAD_DIM : (h + 1) * HEAD_DIM],
                     identity_bf16[:],
                 )
-            return qT_ps
 
-        def keep_queries(t, qT_ps):
-            qT = per_tile.tile([P, HEADS, P], BF16)
-            nc.scalar.copy(
-                out=qT[:].rearrange("d h q -> d (h q)").bitcast(F32),
-                in_=qT_ps[:].rearrange("d h q -> d (h q)").bitcast(F32),
+        def keep_queries(t, qT_ps, heads, copy):
+            if t not in qT_of:
+                qT = per_tile.tile([P, HEADS, P], BF16)
+                qT_of[t] = qT
+            some = slice(heads.start, heads.stop)
+            copy(
+                out=qT_of[t][:, some, :].rearrange("d h q -> d (h q)").bitcast(F32),
+                in_=qT_ps[:, some, :].rearrange("d h q -> d (h q)").bitcast(F32),
             )
-            qT_of[t] = qT
 
         def quantise_values(b):
             v_grouped = per_batch.tile([P, GROUPS * HEAD_DIM, PACK], BF16, align_bytes=64)
@@ -181,25 +178,22 @@ def tile_attention_pb_t_kernel(tc, q_rot, k_rot, v, wo, out):
                 e_sb_of[n] = e_sb
                 eT_ps = eT_banks.tile([P, 2, 2, P], F32)
                 eT_of[n] = eT_ps
-                if n % 2 == 0:
-                    row_sum = per_unit.tile([P, REP], F32)
-                    row_sum_of[n // 2] = row_sum
-            i = 2 * (n % 2) + a
+                if n % UNITS_PER_TILE == 0:
+                    row_sum = per_tile.tile([P, HEADS], F32)
+                    row_sum_of[n // UNITS_PER_TILE] = row_sum
+            head = (n % UNITS_PER_TILE) * 2 + a
             nc.scalar.activation(
                 out=e_sb_of[n][:, a * POSITIONS : (a + 1) * POSITIONS],
                 in_=scores_of[n, a][:],
                 func=EXP,
                 bias=neg_max_of[n][:, a : a + 1],
                 scale=SCALE,
-                accum_out=row_sum_of[n // 2][:, i : i + 1],
+                accum_out=row_sum_of[n // UNITS_PER_TILE][:, head : head + 1],
             )
             e_words = e_sb_of[n][:].bitcast(F32)
             for u in range(2):
                 first = (2 * a + u) * P
                 nc.tensor.transpose(eT_of[n][:, a, u, :], e_words[:, first : first + P], identity_f32[:])
-
-        def leaves_on_vector(n):
-            return n % E_ON_VECTOR_EVERY == E_ON_VECTOR_EVERY - 1
 
         def group_e(n):
             if n % 2 == 0:
@@ -207,10 +201,7 @@ def tile_attention_pb_t_kernel(tc, q_rot, k_rot, v, wo, out):
                 e_grouped_of[n // 2] = e_grouped
             half = slice((n % 2) * POSITIONS, (n % 2 + 1) * POSITIONS)
             grouped_words = e_grouped_of[n // 2][:].bitcast(F32)[:, half].rearrange("p (a q u) -> p a q u", a=2, u=2)
-            if leaves_on_vector(n):
-                nc.vector.tensor_copy(out=grouped_words, in_=eT_of[n][:].rearrange("p a u q -> p a q u"))
-            else:
-                nc.scalar.copy(out=grouped_words, in_=eT_of[n][:].rearrange("p a u q -> p a q u"))
+            nc.scalar.copy(out=grouped_words, in_=eT_of[n][:].rearrange("p a u q -> p a q u"))
 
         def quantise_e(r):
             e_codes = per_unit.tile([P, REP * P], U32, align_bytes=64)
@@ -219,62 +210,47 @@ def tile_attention_pb_t_kernel(tc, q_rot, k_rot, v, wo, out):
             e_codes_of[r] = e_codes
             e_scales_of[r] = e_scales
 
-        def invert_sums(r):
-            inv_sum = per_unit.tile([P, REP], F32)
-            nc.vector.reciprocal(out=inv_sum[:], in_=row_sum_of[r][:])
-            inv_sum_of[r] = inv_sum
+        def spread_factors(t):
+            inv_sum = per_tile.tile([P, HEADS], F32)
+            nc.vector.reciprocal(out=inv_sum[:], in_=row_sum_of[t][:])
+            park = out_rows(t, PARK_ROWS).rearrange("r m -> (r m)")
+            nc.sync.dma_start(out=park.rearrange("(q h) -> q h", h=HEADS), in_=inv_sum[:])
+            factors = per_tile.tile([P, P * HEADS], F32)
+            nc.sync.dma_start(out=factors[:], in_=park.partition_broadcast(P))
+            factors_of[t] = factors
 
         def multiply_by_v(r):
             b = r // (TILES * GROUPS)
             g_cols = slice((r % GROUPS) * HEAD_DIM, (r % GROUPS + 1) * HEAD_DIM)
-            o_ps = o_bank.tile([P, REP, HEAD_DIM], F32)
-            for i in range(REP):
-                q_cols = slice(i * P, (i + 1) * P)
-                nc.tensor.matmul_mx(
-                    out=o_ps[:, i, :],
-                    lhsT=e_codes_of[r][:, q_cols].bitcast(FP8X4),
-                    lhsT_scale=e_scales_of[r][:, q_cols],
-                    rhs=v_codes_of[b][:, g_cols].bitcast(FP8X4),
-                    rhs_scale=v_scales_of[b][:, g_cols],
-                    start=True,
-                    stop=True,
-                )
+            o_ps = o_bank.tile([P, REP, P], F32, tag="o")
+            nc.tensor.matmul_mx(
+                out=o_ps[:].rearrange("d i q -> d (i q)"),
+                lhsT=v_codes_of[b][:, g_cols].bitcast(FP8X4),
+                lhsT_scale=v_scales_of[b][:, g_cols],
+                rhs=e_codes_of[r][:].bitcast(FP8X4),
+                rhs_scale=e_scales_of[r][:],
+                start=True,
+                stop=True,
+            )
             o_ps_of[r] = o_ps
 
         def normalise(r):
             t = r // GROUPS
             g = r % GROUPS
             if g == 0:
-                o_sb = per_tile.tile([P, FEATURES], BF16)
-                o_sb_of[t] = o_sb
+                o_grouped = per_tile.tile([P, GROUPS, P, PACK], BF16, align_bytes=64)
+                o_grouped_of[t] = o_grouped
             nc.vector.tensor_tensor(
-                out=o_sb_of[t][:, g * REP * HEAD_DIM : (g + 1) * REP * HEAD_DIM].rearrange("p (i d) -> p i d", i=REP),
-                in0=o_ps_of[r][:],
-                in1=inv_sum_of[r][:].unsqueeze(2).to_broadcast([P, REP, HEAD_DIM]),
+                out=o_grouped_of[t][:, g, :, :],
+                in0=o_ps_of[r][:].rearrange("d i q -> d q i"),
+                in1=factors_of[t][:].rearrange("d (q h) -> d q h", h=HEADS)[:, :, g * REP : (g + 1) * REP],
                 op=MULT,
             )
-
-        def transpose_o(t):
-            o_words = o_sb_of[t][:].bitcast(F32)
-            oT_ps = side_bank.tile([P, GROUPS, 2, P], F32, tag="side")
-            for g in range(GROUPS):
-                for u in range(2):
-                    first = (2 * g + u) * P
-                    nc.tensor.transpose(oT_ps[:, g, u, :], o_words[:, first : first + P], identity_f32[:])
-            return oT_ps
-
-        def group_o(t, oT_ps):
-            o_grouped = per_tile.tile([P, GROUPS * P * PACK], BF16, align_bytes=64)
-            nc.scalar.copy(
-                out=o_grouped[:].bitcast(F32).rearrange("p (g q u) -> p g q u", g=GROUPS, u=2),
-                in_=oT_ps[:].rearrange("p g u q -> p g q u"),
-            )
-            o_grouped_of[t] = o_grouped
 
         def quantise_o(t):
             o_codes = per_tile.tile([P, GROUPS * P], U32, align_bytes=64)
             o_scales = per_tile.tile([P, GROUPS * P], U8, align_bytes=64)
-            nc.vector.quantize_mx(out=o_codes[:].bitcast(FP8X4), scales=o_scales[:], in_=o_grouped_of[t][:])
+            nc.vector.quantize_mx(out=o_codes[:].bitcast(FP8X4), scales=o_scales[:], in_=o_grouped_of[t][:].rearrange("d g q i -> d (g q i)"))
             o_codes_of[t] = o_codes
             o_scales_of[t] = o_scales
 
@@ -295,46 +271,66 @@ def tile_attention_pb_t_kernel(tc, q_rot, k_rot, v, wo, out):
         def store(t, out_ps):
             out_sb = results.tile([P, MODEL], F32)
             nc.vector.tensor_copy(out=out_sb[:], in_=out_ps[:])
-            nc.sync.dma_start(out=out_rows[t // TILES][:, t % TILES, :], in_=out_sb[:])
+            nc.sync.dma_start(out=out_rows(t, P), in_=out_sb[:])
 
-        keep_keys(0, transpose_keys(0))
-        keep_queries(0, transpose_queries(0))
-        quantise_values(0)
-        for n in range(2):
-            for a in range(2):
-                score_tile(n, a)
-            negate_maxima(n)
-
-        wo_words = wo_sb[:].bitcast(F32)
-        wo_grouped = constants.tile([P, GROUPS * MODEL * PACK], BF16, align_bytes=64)
+        wo_grouped = constants.tile([P, GROUPS, MODEL, PACK], BF16, align_bytes=64)
         wo_codes = constants.tile([P, GROUPS * MODEL], U32, align_bytes=64)
         wo_scales = constants.tile([P, GROUPS * MODEL], U8, align_bytes=64)
-        for g in range(GROUPS):
-            eT_ps = eT_banks.tile([P, 2, 2, P], F32)
-            for u in range(2):
+
+        def transpose_wo(g):
+            wo_ps = o_bank.tile([P, REP, 2, P], BF16, tag="o")
+            for i in range(REP):
                 for a in range(2):
-                    first = a * (FEATURES // 2) + (2 * g + u) * P
-                    nc.tensor.transpose(eT_ps[:, u, a, :], wo_words[:, first : first + P], identity_f32[:])
-            nc.vector.tensor_copy(
-                out=wo_grouped[:].bitcast(F32)[:, g * 2 * MODEL : (g + 1) * 2 * MODEL].rearrange(
-                    "p (m u) -> p m u", u=2
-                ),
-                in_=eT_ps[:].rearrange("p u a m -> p (a m) u"),
+                    first = a * FEATURES + (g * REP + i) * HEAD_DIM
+                    nc.tensor.transpose(wo_ps[:, i, a, :], wo_sb[:, first : first + HEAD_DIM], identity_bf16[:])
+            return wo_ps
+
+        def group_wo(g, wo_ps):
+            nc.vector.tensor_copy(out=wo_grouped[:, g, :, :], in_=wo_ps[:].rearrange("d i a m -> d (a m) i"))
+
+        def quantise_wo():
+            nc.vector.quantize_mx(
+                out=wo_codes[:].bitcast(FP8X4), scales=wo_scales[:], in_=wo_grouped[:].rearrange("d g m i -> d (g m i)")
             )
-        nc.vector.quantize_mx(out=wo_codes[:].bitcast(FP8X4), scales=wo_scales[:], in_=wo_grouped[:])
+
+        all_groups, all_heads = range(GROUPS), range(HEADS)
+        first_kT_ps = side_bank.tile([P, GROUPS, TILES, P], BF16, tag="side")
+        first_qT_ps = o_bank.tile([P, HEADS, P], BF16, tag="o")
+        transpose_keys(0, first_kT_ps, range(1))
+        keep_keys(0, first_kT_ps, range(1), nc.vector.tensor_copy)
+        transpose_queries(0, first_qT_ps, range(REP))
+        keep_queries(0, first_qT_ps, range(REP), nc.scalar.copy)
+        for a in range(2):
+            score_tile(0, a)
+        negate_maxima(0)
+        transpose_keys(0, first_kT_ps, range(1, GROUPS))
+        keep_keys(0, first_kT_ps, range(1, GROUPS), nc.vector.tensor_copy)
+        transpose_queries(0, first_qT_ps, range(REP, HEADS))
+        keep_queries(0, first_qT_ps, range(REP, HEADS), nc.vector.tensor_copy)
+        for a in range(2):
+            score_tile(1, a)
+        negate_maxima(1)
 
         side_ps = None
-        for n in range(n_units + 8):
+        wo_ps = None
+        for n in range(n_units + 9):
             phase = n % UNITS_PER_TILE
             t = n // UNITS_PER_TILE
-            r = (n - 2) // 2
-            round_ready = n % 2 == 1 and 0 <= r < n_tiles * GROUPS
+            r = (n - 7) // 2
+            divides = n % 2 == 1 and 0 <= r < n_tiles * GROUPS
             new_batch = (t + 2) % TILES == 0 and t + 2 < n_tiles
 
-            if 1 <= n <= n_units and leaves_on_vector(n - 1):
-                group_e(n - 1)
-            if phase == 2 and 0 <= t - 2 < n_tiles:
-                store(t - 2, side_ps)
+            if phase == 1 and t // TILES + 1 < BATCH:
+                if t % TILES == 0:
+                    load_keys(t // TILES + 1)
+                load_queries(t // TILES + 1, t % TILES)
+                if t % TILES == 1:
+                    load_values(t // TILES + 1)
+
+            if phase == 0 and 0 <= t - 1 < n_tiles:
+                spread_factors(t - 1)
+            if phase == 0 and 0 <= t - 3 < n_tiles:
+                store(t - 3, side_ps)
 
             for a in range(2):
                 if n < n_units:
@@ -344,32 +340,37 @@ def tile_attention_pb_t_kernel(tc, q_rot, k_rot, v, wo, out):
             if n + 2 < n_units:
                 negate_maxima(n + 2)
 
-            if 1 <= n <= n_units and not leaves_on_vector(n - 1):
+            if 1 <= n <= n_units:
                 group_e(n - 1)
-            if phase == 0 and 0 <= t - 2 < n_tiles:
-                group_o(t - 2, side_ps)
             if phase == 1 and t + 1 < n_tiles:
-                keep_queries(t + 1, side_ps)
+                keep_queries(t + 1, side_ps, all_heads, nc.scalar.copy)
             if phase == 3 and new_batch:
-                keep_keys((t + 2) // TILES, side_ps)
+                keep_keys((t + 2) // TILES, side_ps, all_groups, nc.scalar.copy)
 
-            if round_ready:
+            if divides:
                 multiply_by_v(r)
             if n % 2 == 0 and 2 <= n <= n_units:
                 quantise_e((n - 2) // 2)
-                invert_sums((n - 2) // 2)
-            if phase == 0 and 0 <= t - 2 < n_tiles:
+            if phase == 2 and 0 <= t - 2 < n_tiles:
                 quantise_o(t - 2)
             if phase == 2 and new_batch:
                 quantise_values((t + 2) // TILES)
-            if round_ready:
+            if divides:
                 normalise(r)
+            if n in (1, 3):
+                wo_ps = transpose_wo(n // 2)
+            if n in (2, 4):
+                group_wo(n // 2 - 1, wo_ps)
+            if n == 3:
+                quantise_values(0)
+            if n == 5:
+                quantise_wo()
 
             if phase == 0 and t + 1 < n_tiles:
-                side_ps = transpose_queries(t + 1)
-            if phase == 1 and 0 <= t - 2 < n_tiles:
-                side_ps = project(t - 2)
+                side_ps = side_bank.tile([P, HEADS, P], BF16, tag="side")
+                transpose_queries(t + 1, side_ps, all_heads)
             if phase == 2 and new_batch:
-                side_ps = transpose_keys((t + 2) // TILES)
-            if phase == 3 and 0 <= t - 1 < n_tiles:
-                side_ps = transpose_o(t - 1)
+                side_ps = side_bank.tile([P, GROUPS, TILES, P], BF16, tag="side")
+                transpose_keys((t + 2) // TILES, side_ps, all_groups)
+            if phase == 3 and 0 <= t - 2 < n_tiles:
+                side_ps = project(t - 2)

@@ -167,17 +167,18 @@ def tile_attention_pb_t_kernel(tc, q_rot, k_rot, v, wo, out):
             nc.vector.reduce_max(out=row_max_of[n][:, a : a + 1], in_=s_ps[:], axis=ALONG_ROW)
             scores_of[n, a] = s_ps
 
-        def negate_maxima(n):
-            neg_max = per_unit.tile([P, 2], F32)
-            nc.gpsimd.tensor_scalar_mul(out=neg_max[:], in0=row_max_of[n][:], scalar1=-SCALE)
-            neg_max_of[n] = neg_max
+        def negate_maxima(n, a):
+            if a == 0:
+                neg_max = per_unit.tile([P, 2], F32)
+                neg_max_of[n] = neg_max
+            nc.gpsimd.tensor_scalar_mul(
+                out=neg_max_of[n][:, a : a + 1], in0=row_max_of[n][:, a : a + 1], scalar1=-SCALE
+            )
 
         def exponential(n, a):
             if a == 0:
                 e_sb = per_unit.tile([P, 2 * POSITIONS], BF16)
                 e_sb_of[n] = e_sb
-                eT_ps = eT_banks.tile([P, 2, 2, P], F32)
-                eT_of[n] = eT_ps
                 if n % UNITS_PER_TILE == 0:
                     row_sum = per_tile.tile([P, HEADS], F32)
                     row_sum_of[n // UNITS_PER_TILE] = row_sum
@@ -190,6 +191,11 @@ def tile_attention_pb_t_kernel(tc, q_rot, k_rot, v, wo, out):
                 scale=SCALE,
                 accum_out=row_sum_of[n // UNITS_PER_TILE][:, head : head + 1],
             )
+
+        def transpose_e(n, a):
+            if a == 0:
+                eT_ps = eT_banks.tile([P, 2, 2, P], F32)
+                eT_of[n] = eT_ps
             e_words = e_sb_of[n][:].bitcast(F32)
             for u in range(2):
                 first = (2 * a + u) * P
@@ -302,14 +308,14 @@ def tile_attention_pb_t_kernel(tc, q_rot, k_rot, v, wo, out):
         keep_queries(0, first_qT_ps, range(REP), nc.scalar.copy)
         for a in range(2):
             score_tile(0, a)
-        negate_maxima(0)
+            negate_maxima(0, a)
         transpose_keys(0, first_kT_ps, range(1, GROUPS))
         keep_keys(0, first_kT_ps, range(1, GROUPS), nc.vector.tensor_copy)
         transpose_queries(0, first_qT_ps, range(REP, HEADS))
         keep_queries(0, first_qT_ps, range(REP, HEADS), nc.vector.tensor_copy)
         for a in range(2):
             score_tile(1, a)
-        negate_maxima(1)
+            negate_maxima(1, a)
 
         side_ps = None
         wo_ps = None
@@ -337,8 +343,9 @@ def tile_attention_pb_t_kernel(tc, q_rot, k_rot, v, wo, out):
                     exponential(n, a)
                 if n + 2 < n_units:
                     score_tile(n + 2, a)
-            if n + 2 < n_units:
-                negate_maxima(n + 2)
+                    negate_maxima(n + 2, a)
+                if n < n_units:
+                    transpose_e(n, a)
 
             if 1 <= n <= n_units:
                 group_e(n - 1)

@@ -11,6 +11,7 @@ FP8X4 = mybir.dt.float8_e4m3fn_x4
 EXP = mybir.ActivationFunctionType.Exp
 ALONG_ROW = mybir.AxisListType.X
 MULT = mybir.AluOpType.mult
+ADD = mybir.AluOpType.add
 
 P = 128
 PACK = 4
@@ -25,6 +26,7 @@ FEATURES = HEADS * HEAD_DIM
 MODEL = 256
 SCALE = HEAD_DIM ** -0.5
 UNITS_PER_TILE = 4
+VALUE_PIECES = 8
 PARK_ROWS = P * HEADS // MODEL
 
 FLOPS = 2 * BATCH * HEADS * POSITIONS * POSITIONS * HEAD_DIM * 2 + 2 * BATCH * POSITIONS * FEATURES * MODEL
@@ -99,7 +101,7 @@ def tile_attention_pb_t_kernel(tc, q_rot, k_rot, v, wo, out):
         one = constants.tile([P, 1], F32)
         nc.scalar.activation(out=one[:], in_=zero[:], func=EXP)
 
-        kT_of, v_codes_of, v_scales_of = {}, {}, {}
+        kT_of, v_grouped_of, v_codes_of, v_scales_of = {}, {}, {}, {}
         qT_of, o_grouped_of, o_codes_of, o_scales_of = {}, {}, {}, {}
         row_sum_of, factors_of, o_ps_of = {}, {}, {}
         row_max_of, neg_max_of, scores_of, e_sb_of, eT_of, e_grouped_of, e_codes_of, e_scales_of = (
@@ -141,15 +143,28 @@ def tile_attention_pb_t_kernel(tc, q_rot, k_rot, v, wo, out):
                 in_=qT_ps[:, some, :].rearrange("d h q -> d (h q)").bitcast(F32),
             )
 
+        def group_values(b, piece):
+            if piece == 0:
+                v_grouped = per_batch.tile([P, GROUPS * HEAD_DIM, PACK], BF16, align_bytes=64)
+                v_grouped_of[b] = v_grouped
+            width = GROUPS * HEAD_DIM // VALUE_PIECES
+            cols = slice(piece * width, (piece + 1) * width)
+            nc.gpsimd.tensor_scalar(
+                out=v_grouped_of[b][:, cols, :],
+                in0=v_sb[b][:, :, cols].rearrange("p t c -> p c t"),
+                scalar1=1.0,
+                scalar2=0.0,
+                op0=MULT,
+                op1=ADD,
+            )
+
         def quantise_values(b):
-            v_grouped = per_batch.tile([P, GROUPS * HEAD_DIM, PACK], BF16, align_bytes=64)
-            nc.vector.tensor_copy(out=v_grouped[:], in_=v_sb[b][:].rearrange("p t c -> p c t"))
             v_codes = per_batch.tile([P, GROUPS * HEAD_DIM], U32, align_bytes=64)
             v_scales = per_batch.tile([P, GROUPS * HEAD_DIM], U8, align_bytes=64)
             nc.vector.quantize_mx(
                 out=v_codes[:].bitcast(FP8X4),
                 scales=v_scales[:],
-                in_=v_grouped[:].rearrange("p c t -> p (c t)"),
+                in_=v_grouped_of[b][:].rearrange("p c t -> p (c t)"),
             )
             v_codes_of[b] = v_codes
             v_scales_of[b] = v_scales
@@ -160,7 +175,7 @@ def tile_attention_pb_t_kernel(tc, q_rot, k_rot, v, wo, out):
             if a == 0:
                 row_max = per_unit.tile([P, 2], F32)
                 row_max_of[n] = row_max
-            s_ps = score_banks.tile([P, POSITIONS], F32)
+            s_ps = score_banks.tile([P, POSITIONS], F32, tag="scores")
             nc.tensor.matmul(
                 out=s_ps[:], lhsT=qT_of[t][:, head, :], rhs=kT_of[t // TILES][:, head // REP, :], start=True, stop=True
             )
@@ -201,20 +216,28 @@ def tile_attention_pb_t_kernel(tc, q_rot, k_rot, v, wo, out):
                 first = (2 * a + u) * P
                 nc.tensor.transpose(eT_of[n][:, a, u, :], e_words[:, first : first + P], identity_f32[:])
 
-        def group_e(n):
-            if n % 2 == 0:
-                e_grouped = per_unit.tile([P, REP * P * PACK], BF16, align_bytes=64)
+        def group_e(n, heads, copy):
+            if n % 2 == 0 and heads.start == 0:
+                e_grouped = per_unit.tile([P, REP, P, 2], F32, align_bytes=64)
                 e_grouped_of[n // 2] = e_grouped
-            half = slice((n % 2) * POSITIONS, (n % 2 + 1) * POSITIONS)
-            grouped_words = e_grouped_of[n // 2][:].bitcast(F32)[:, half].rearrange("p (a q u) -> p a q u", a=2, u=2)
-            nc.scalar.copy(out=grouped_words, in_=eT_of[n][:].rearrange("p a u q -> p a q u"))
+            first = (n % 2) * 2
+            copy(
+                out=e_grouped_of[n // 2][:, first + heads.start : first + heads.stop, :, :],
+                in_=eT_of[n][:, heads.start : heads.stop, :, :].rearrange("p a u q -> p a q u"),
+            )
 
-        def quantise_e(r):
-            e_codes = per_unit.tile([P, REP * P], U32, align_bytes=64)
-            e_scales = per_unit.tile([P, REP * P], U8, align_bytes=64)
-            nc.vector.quantize_mx(out=e_codes[:].bitcast(FP8X4), scales=e_scales[:], in_=e_grouped_of[r][:])
-            e_codes_of[r] = e_codes
-            e_scales_of[r] = e_scales
+        def quantise_e(r, heads):
+            if heads.start == 0:
+                e_codes = per_unit.tile([P, REP * P], U32, align_bytes=64)
+                e_scales = per_unit.tile([P, REP * P], U8, align_bytes=64)
+                e_codes_of[r] = e_codes
+                e_scales_of[r] = e_scales
+            cols = slice(heads.start * P, heads.stop * P)
+            nc.vector.quantize_mx(
+                out=e_codes_of[r][:, cols].bitcast(FP8X4),
+                scales=e_scales_of[r][:, cols],
+                in_=e_grouped_of[r][:, heads.start : heads.stop, :, :].rearrange("p i q u -> p (i q u)").bitcast(BF16),
+            )
 
         def spread_factors(t):
             inv_sum = per_tile.tile([P, HEADS], F32)
@@ -223,18 +246,33 @@ def tile_attention_pb_t_kernel(tc, q_rot, k_rot, v, wo, out):
             nc.sync.dma_start(out=park.rearrange("(q h) -> q h", h=HEADS), in_=inv_sum[:])
             factors = per_tile.tile([P, P * HEADS], F32)
             nc.sync.dma_start(out=factors[:], in_=park.partition_broadcast(P))
-            factors_of[t] = factors
+            for g in range(GROUPS):
+                factors_of[2 * t + g] = factors[:].rearrange("d (q h) -> d q h", h=HEADS)[:, :, g * REP : (g + 1) * REP]
 
-        def multiply_by_v(r):
+        def turn_factors(r):
+            inv_sum = per_tile.tile([P, REP], F32)
+            group = slice((r % GROUPS) * REP, (r % GROUPS + 1) * REP)
+            nc.vector.reciprocal(out=inv_sum[:], in_=row_sum_of[r // GROUPS][:, group])
+            factors_ps = score_banks.tile([P, REP, P], F32, tag="scores")
+            for i in range(REP):
+                nc.tensor.transpose(factors_ps[:, i, :], inv_sum[:, i : i + 1].to_broadcast([P, P]), identity_f32[:])
+            return factors_ps
+
+        def keep_factors(r, factors_ps, copy):
+            round_factors = per_tile.tile([P, REP, P], F32)
+            copy(out=round_factors[:], in_=factors_ps[:])
+            factors_of[r] = round_factors[:].rearrange("d i q -> d q i")
+
+        def multiply_by_v(r, o_ps, heads):
             b = r // (TILES * GROUPS)
             g_cols = slice((r % GROUPS) * HEAD_DIM, (r % GROUPS + 1) * HEAD_DIM)
-            o_ps = o_bank.tile([P, REP, P], F32, tag="o")
+            q_cols = slice(heads.start * P, heads.stop * P)
             nc.tensor.matmul_mx(
-                out=o_ps[:].rearrange("d i q -> d (i q)"),
+                out=o_ps[:, q_cols],
                 lhsT=v_codes_of[b][:, g_cols].bitcast(FP8X4),
                 lhsT_scale=v_scales_of[b][:, g_cols],
-                rhs=e_codes_of[r][:].bitcast(FP8X4),
-                rhs_scale=e_scales_of[r][:],
+                rhs=e_codes_of[r][:, q_cols].bitcast(FP8X4),
+                rhs_scale=e_scales_of[r][:, q_cols],
                 start=True,
                 stop=True,
             )
@@ -248,21 +286,26 @@ def tile_attention_pb_t_kernel(tc, q_rot, k_rot, v, wo, out):
                 o_grouped_of[t] = o_grouped
             nc.vector.tensor_tensor(
                 out=o_grouped_of[t][:, g, :, :],
-                in0=o_ps_of[r][:].rearrange("d i q -> d q i"),
-                in1=factors_of[t][:].rearrange("d (q h) -> d q h", h=HEADS)[:, :, g * REP : (g + 1) * REP],
+                in0=o_ps_of[r][:].rearrange("d (i q) -> d q i", i=REP),
+                in1=factors_of[r],
                 op=MULT,
             )
 
-        def quantise_o(t):
-            o_codes = per_tile.tile([P, GROUPS * P], U32, align_bytes=64)
-            o_scales = per_tile.tile([P, GROUPS * P], U8, align_bytes=64)
-            nc.vector.quantize_mx(out=o_codes[:].bitcast(FP8X4), scales=o_scales[:], in_=o_grouped_of[t][:].rearrange("d g q i -> d (g q i)"))
-            o_codes_of[t] = o_codes
-            o_scales_of[t] = o_scales
+        def quantise_o(t, groups):
+            if groups.start == 0:
+                o_codes = per_tile.tile([P, GROUPS * P], U32, align_bytes=64)
+                o_scales = per_tile.tile([P, GROUPS * P], U8, align_bytes=64)
+                o_codes_of[t] = o_codes
+                o_scales_of[t] = o_scales
+            cols = slice(groups.start * P, groups.stop * P)
+            nc.vector.quantize_mx(
+                out=o_codes_of[t][:, cols].bitcast(FP8X4),
+                scales=o_scales_of[t][:, cols],
+                in_=o_grouped_of[t][:, groups.start : groups.stop, :, :].rearrange("d g q i -> d (g q i)"),
+            )
 
-        def project(t):
-            out_ps = side_bank.tile([P, MODEL], F32, tag="side")
-            for g in range(GROUPS):
+        def project(t, out_ps, groups):
+            for g in groups:
                 nc.tensor.matmul_mx(
                     out=out_ps[:],
                     lhsT=o_codes_of[t][:, g * P : (g + 1) * P].bitcast(FP8X4),
@@ -272,11 +315,12 @@ def tile_attention_pb_t_kernel(tc, q_rot, k_rot, v, wo, out):
                     start=(g == 0),
                     stop=(g == GROUPS - 1),
                 )
-            return out_ps
 
-        def store(t, out_ps):
+        def store(t, out_ps, copies):
             out_sb = results.tile([P, MODEL], F32)
-            nc.vector.tensor_copy(out=out_sb[:], in_=out_ps[:])
+            width = MODEL // len(copies)
+            for c, copy in enumerate(copies):
+                copy(out=out_sb[:, c * width : (c + 1) * width], in_=out_ps[:, c * width : (c + 1) * width])
             nc.sync.dma_start(out=out_rows(t, P), in_=out_sb[:])
 
         wo_grouped = constants.tile([P, GROUPS, MODEL, PACK], BF16, align_bytes=64)
@@ -299,7 +343,9 @@ def tile_attention_pb_t_kernel(tc, q_rot, k_rot, v, wo, out):
                 out=wo_codes[:].bitcast(FP8X4), scales=wo_scales[:], in_=wo_grouped[:].rearrange("d g m i -> d (g m i)")
             )
 
-        all_groups, all_heads = range(GROUPS), range(HEADS)
+        all_groups, all_heads, unit_heads, round_heads = (
+            range(GROUPS), range(HEADS), range(2), range(REP),
+        )
         first_kT_ps = side_bank.tile([P, GROUPS, TILES, P], BF16, tag="side")
         first_qT_ps = o_bank.tile([P, HEADS, P], BF16, tag="o")
         transpose_keys(0, first_kT_ps, range(1))
@@ -319,11 +365,11 @@ def tile_attention_pb_t_kernel(tc, q_rot, k_rot, v, wo, out):
 
         side_ps = None
         wo_ps = None
-        for n in range(n_units + 9):
+        for n in range(n_units - 2):
             phase = n % UNITS_PER_TILE
             t = n // UNITS_PER_TILE
             r = (n - 7) // 2
-            divides = n % 2 == 1 and 0 <= r < n_tiles * GROUPS
+            divides = n % 2 == 1 and 0 <= r
             new_batch = (t + 2) % TILES == 0 and t + 2 < n_tiles
 
             if phase == 1 and t // TILES + 1 < BATCH:
@@ -333,44 +379,47 @@ def tile_attention_pb_t_kernel(tc, q_rot, k_rot, v, wo, out):
                 if t % TILES == 1:
                     load_values(t // TILES + 1)
 
-            if phase == 0 and 0 <= t - 1 < n_tiles:
+            if phase == 0 and 0 <= t - 1:
                 spread_factors(t - 1)
-            if phase == 0 and 0 <= t - 3 < n_tiles:
-                store(t - 3, side_ps)
+            if phase == 0 and 0 <= t - 3:
+                store(t - 3, side_ps, [nc.vector.tensor_copy])
 
             for a in range(2):
-                if n < n_units:
-                    exponential(n, a)
-                if n + 2 < n_units:
-                    score_tile(n + 2, a)
-                    negate_maxima(n + 2, a)
-                if n < n_units:
-                    transpose_e(n, a)
+                exponential(n, a)
+                score_tile(n + 2, a)
+                negate_maxima(n + 2, a)
+                transpose_e(n, a)
+                b, piece = (t + 1) // TILES, phase * 2 + a
+                if n < UNITS_PER_TILE:
+                    group_values(0, piece)
+                elif (t + 1) % TILES == 0 and b < BATCH:
+                    group_values(b, piece)
 
-            if 1 <= n <= n_units:
-                group_e(n - 1)
+            if 1 <= n:
+                group_e(n - 1, unit_heads, nc.scalar.copy)
             if phase == 1 and t + 1 < n_tiles:
                 keep_queries(t + 1, side_ps, all_heads, nc.scalar.copy)
             if phase == 3 and new_batch:
                 keep_keys((t + 2) // TILES, side_ps, all_groups, nc.scalar.copy)
 
             if divides:
-                multiply_by_v(r)
-            if n % 2 == 0 and 2 <= n <= n_units:
-                quantise_e((n - 2) // 2)
-            if phase == 2 and 0 <= t - 2 < n_tiles:
-                quantise_o(t - 2)
-            if phase == 2 and new_batch:
-                quantise_values((t + 2) // TILES)
+                o_ps = o_bank.tile([P, REP * P], F32, tag="o")
+                multiply_by_v(r, o_ps, round_heads)
+            if n % 2 == 0 and 2 <= n:
+                quantise_e((n - 2) // 2, round_heads)
+            if phase == 2 and 0 <= t - 2:
+                quantise_o(t - 2, all_groups)
+            if phase == 0 and t % TILES == 0 and t > 0:
+                quantise_values(t // TILES)
             if divides:
                 normalise(r)
             if n in (1, 3):
                 wo_ps = transpose_wo(n // 2)
             if n in (2, 4):
                 group_wo(n // 2 - 1, wo_ps)
-            if n == 3:
-                quantise_values(0)
             if n == 5:
+                quantise_values(0)
+            if n == 6:
                 quantise_wo()
 
             if phase == 0 and t + 1 < n_tiles:
@@ -379,5 +428,53 @@ def tile_attention_pb_t_kernel(tc, q_rot, k_rot, v, wo, out):
             if phase == 2 and new_batch:
                 side_ps = side_bank.tile([P, GROUPS, TILES, P], BF16, tag="side")
                 transpose_keys((t + 2) // TILES, side_ps, all_groups)
-            if phase == 3 and 0 <= t - 2 < n_tiles:
-                side_ps = project(t - 2)
+            if phase == 3 and 0 <= t - 2:
+                side_ps = side_bank.tile([P, MODEL], F32, tag="side")
+                project(t - 2, side_ps, all_groups)
+
+        n, t, r = n_units - 1, n_tiles - 1, n_tiles * GROUPS - 1
+        exponential(n - 1, 0)
+        factors_ps = turn_factors(r - 1)
+        transpose_e(n - 1, 0)
+        exponential(n - 1, 1)
+        group_e(n - 2, unit_heads, nc.scalar.copy)
+        transpose_e(n - 1, 1)
+        quantise_o(t - 2, all_groups)
+        side_ps = side_bank.tile([P, MODEL], F32, tag="side")
+        project(t - 2, side_ps, all_groups)
+        keep_factors(r - 1, factors_ps, nc.vector.tensor_copy)
+        quantise_e(r - 1, round_heads)
+        store(t - 2, side_ps, [nc.vector.tensor_copy])
+
+        exponential(n, 0)
+        transpose_e(n, 0)
+        exponential(n, 1)
+        group_e(n - 1, unit_heads, nc.scalar.copy)
+        o_ps = o_bank.tile([P, REP * P], F32, tag="o")
+        multiply_by_v(r - 3, o_ps, round_heads)
+        normalise(r - 3)
+        o_ps = score_banks.tile([P, REP * P], F32, tag="scores")
+        multiply_by_v(r - 2, o_ps, round_heads)
+        transpose_e(n, 1)
+        group_e(n, unit_heads, nc.scalar.copy)
+        o_ps = score_banks.tile([P, REP * P], F32, tag="scores")
+        multiply_by_v(r - 1, o_ps, round_heads)
+        factors_ps = turn_factors(r)
+        keep_factors(r, factors_ps, nc.scalar.copy)
+        quantise_e(r, range(2))
+        normalise(r - 2)
+        o_ps = score_banks.tile([P, REP * P], F32, tag="scores")
+        multiply_by_v(r, o_ps, range(2))
+        quantise_e(r, range(2, REP))
+        multiply_by_v(r, o_ps, range(2, REP))
+        normalise(r - 1)
+        quantise_o(t - 1, all_groups)
+        normalise(r)
+        side_ps = side_bank.tile([P, MODEL], F32, tag="side")
+        project(t - 1, side_ps, all_groups)
+        store(t - 1, side_ps, [nc.scalar.copy])
+        quantise_o(t, range(1))
+        quantise_o(t, range(1, GROUPS))
+        side_ps = side_bank.tile([P, MODEL], F32, tag="side")
+        project(t, side_ps, all_groups)
+        store(t, side_ps, [nc.vector.tensor_copy, nc.scalar.copy])

@@ -278,16 +278,17 @@ def tile_attention_pb_t_kernel(tc, q_rot, k_rot, v, wo, out):
             )
             o_ps_of[r] = o_ps
 
-        def normalise(r):
+        def normalise(r, queries):
             t = r // GROUPS
             g = r % GROUPS
-            if g == 0:
+            if g == 0 and queries.start == 0:
                 o_grouped = per_tile.tile([P, GROUPS, P, PACK], BF16, align_bytes=64)
                 o_grouped_of[t] = o_grouped
+            some = slice(queries.start, queries.stop)
             nc.vector.tensor_tensor(
-                out=o_grouped_of[t][:, g, :, :],
-                in0=o_ps_of[r][:].rearrange("d (i q) -> d q i", i=REP),
-                in1=factors_of[r],
+                out=o_grouped_of[t][:, g, some, :],
+                in0=o_ps_of[r][:].rearrange("d (i q) -> d q i", i=REP)[:, some, :],
+                in1=factors_of[r][:, some, :],
                 op=MULT,
             )
 
@@ -343,9 +344,8 @@ def tile_attention_pb_t_kernel(tc, q_rot, k_rot, v, wo, out):
                 out=wo_codes[:].bitcast(FP8X4), scales=wo_scales[:], in_=wo_grouped[:].rearrange("d g m i -> d (g m i)")
             )
 
-        all_groups, all_heads, unit_heads, round_heads = (
-            range(GROUPS), range(HEADS), range(2), range(REP),
-        )
+        all_groups, group_0_heads, group_1_heads = range(GROUPS), range(REP), range(REP, HEADS)
+        unit_heads, round_heads, all_queries = range(2), range(REP), range(P)
         first_kT_ps = side_bank.tile([P, GROUPS, TILES, P], BF16, tag="side")
         first_qT_ps = o_bank.tile([P, HEADS, P], BF16, tag="o")
         transpose_keys(0, first_kT_ps, range(1))
@@ -368,8 +368,6 @@ def tile_attention_pb_t_kernel(tc, q_rot, k_rot, v, wo, out):
         for n in range(n_units - 2):
             phase = n % UNITS_PER_TILE
             t = n // UNITS_PER_TILE
-            r = (n - 7) // 2
-            divides = n % 2 == 1 and 0 <= r
             new_batch = (t + 2) % TILES == 0 and t + 2 < n_tiles
 
             if phase == 1 and t // TILES + 1 < BATCH:
@@ -398,21 +396,24 @@ def tile_attention_pb_t_kernel(tc, q_rot, k_rot, v, wo, out):
             if 1 <= n:
                 group_e(n - 1, unit_heads, nc.scalar.copy)
             if phase == 1 and t + 1 < n_tiles:
-                keep_queries(t + 1, side_ps, all_heads, nc.scalar.copy)
+                keep_queries(t + 1, side_ps, group_0_heads, nc.scalar.copy)
+            if phase == 2 and t + 1 < n_tiles:
+                keep_queries(t + 1, side_ps, group_1_heads, nc.scalar.copy)
             if phase == 3 and new_batch:
                 keep_keys((t + 2) // TILES, side_ps, all_groups, nc.scalar.copy)
 
-            if divides:
+            if n % 2 == 1 and 7 <= n:
                 o_ps = o_bank.tile([P, REP * P], F32, tag="o")
-                multiply_by_v(r, o_ps, round_heads)
-            if n % 2 == 0 and 2 <= n:
-                quantise_e((n - 2) // 2, round_heads)
+                multiply_by_v((n - 7) // 2, o_ps, round_heads)
+            if 7 <= n:
+                h = (n - 7) % 2
+                normalise((n - 7) // 2, range(h * P // 2, (h + 1) * P // 2))
+            if 2 <= n:
+                quantise_e((n - 2) // 2, range(n % 2 * 2, n % 2 * 2 + 2))
             if phase == 2 and 0 <= t - 2:
                 quantise_o(t - 2, all_groups)
             if phase == 0 and t % TILES == 0 and t > 0:
                 quantise_values(t // TILES)
-            if divides:
-                normalise(r)
             if n in (1, 3):
                 wo_ps = transpose_wo(n // 2)
             if n in (2, 4):
@@ -424,7 +425,10 @@ def tile_attention_pb_t_kernel(tc, q_rot, k_rot, v, wo, out):
 
             if phase == 0 and t + 1 < n_tiles:
                 side_ps = side_bank.tile([P, HEADS, P], BF16, tag="side")
-                transpose_queries(t + 1, side_ps, all_heads)
+                transpose_queries(t + 1, side_ps, group_0_heads)
+            if phase == 1 and t + 1 < n_tiles:
+                side_ps = side_bank.tile([P, HEADS, P], BF16, tag="side")
+                transpose_queries(t + 1, side_ps, group_1_heads)
             if phase == 2 and new_batch:
                 side_ps = side_bank.tile([P, GROUPS, TILES, P], BF16, tag="side")
                 transpose_keys((t + 2) // TILES, side_ps, all_groups)
@@ -439,6 +443,7 @@ def tile_attention_pb_t_kernel(tc, q_rot, k_rot, v, wo, out):
         exponential(n - 1, 1)
         group_e(n - 2, unit_heads, nc.scalar.copy)
         transpose_e(n - 1, 1)
+        normalise(r - 4, range(P // 2, P))
         quantise_o(t - 2, all_groups)
         side_ps = side_bank.tile([P, MODEL], F32, tag="side")
         project(t - 2, side_ps, all_groups)
@@ -452,7 +457,7 @@ def tile_attention_pb_t_kernel(tc, q_rot, k_rot, v, wo, out):
         group_e(n - 1, unit_heads, nc.scalar.copy)
         o_ps = o_bank.tile([P, REP * P], F32, tag="o")
         multiply_by_v(r - 3, o_ps, round_heads)
-        normalise(r - 3)
+        normalise(r - 3, all_queries)
         o_ps = score_banks.tile([P, REP * P], F32, tag="scores")
         multiply_by_v(r - 2, o_ps, round_heads)
         transpose_e(n, 1)
@@ -462,14 +467,14 @@ def tile_attention_pb_t_kernel(tc, q_rot, k_rot, v, wo, out):
         factors_ps = turn_factors(r)
         keep_factors(r, factors_ps, nc.scalar.copy)
         quantise_e(r, range(2))
-        normalise(r - 2)
+        normalise(r - 2, all_queries)
         o_ps = score_banks.tile([P, REP * P], F32, tag="scores")
         multiply_by_v(r, o_ps, range(2))
         quantise_e(r, range(2, REP))
         multiply_by_v(r, o_ps, range(2, REP))
-        normalise(r - 1)
+        normalise(r - 1, all_queries)
         quantise_o(t - 1, all_groups)
-        normalise(r)
+        normalise(r, all_queries)
         side_ps = side_bank.tile([P, MODEL], F32, tag="side")
         project(t - 1, side_ps, all_groups)
         store(t - 1, side_ps, [nc.scalar.copy])

@@ -27,6 +27,7 @@ MODEL = 256
 SCALE = HEAD_DIM ** -0.5
 UNITS_PER_TILE = 4
 VALUE_PIECES = 8
+WARM_UP = 5
 PARK_ROWS = P * HEADS // MODEL
 
 FLOPS = 2 * BATCH * HEADS * POSITIONS * POSITIONS * HEAD_DIM * 2 + 2 * BATCH * POSITIONS * FEATURES * MODEL
@@ -100,6 +101,12 @@ def tile_attention_pb_t_kernel(tc, q_rot, k_rot, v, wo, out):
         nc.vector.memset(zero[:], 0.0)
         one = constants.tile([P, 1], F32)
         nc.scalar.activation(out=one[:], in_=zero[:], func=EXP)
+
+        zeros = constants.tile([P, POSITIONS], BF16)
+        nc.vector.memset(zeros[:], 0.0)
+        warm_ps = score_banks.tile([P, POSITIONS], F32, tag="scores")
+        for i in range(WARM_UP):
+            nc.tensor.matmul(out=warm_ps[:], lhsT=zeros[:, :P], rhs=zeros[:], start=True, stop=True)
 
         kT_of, v_grouped_of, v_codes_of, v_scales_of = {}, {}, {}, {}
         qT_of, o_grouped_of, o_codes_of, o_scales_of = {}, {}, {}, {}
@@ -278,17 +285,16 @@ def tile_attention_pb_t_kernel(tc, q_rot, k_rot, v, wo, out):
             )
             o_ps_of[r] = o_ps
 
-        def normalise(r, queries):
+        def normalise(r):
             t = r // GROUPS
             g = r % GROUPS
-            if g == 0 and queries.start == 0:
+            if g == 0:
                 o_grouped = per_tile.tile([P, GROUPS, P, PACK], BF16, align_bytes=64)
                 o_grouped_of[t] = o_grouped
-            some = slice(queries.start, queries.stop)
             nc.vector.tensor_tensor(
-                out=o_grouped_of[t][:, g, some, :],
-                in0=o_ps_of[r][:].rearrange("d (i q) -> d q i", i=REP)[:, some, :],
-                in1=factors_of[r][:, some, :],
+                out=o_grouped_of[t][:, g, :, :],
+                in0=o_ps_of[r][:].rearrange("d (i q) -> d q i", i=REP),
+                in1=factors_of[r],
                 op=MULT,
             )
 
@@ -345,23 +351,22 @@ def tile_attention_pb_t_kernel(tc, q_rot, k_rot, v, wo, out):
             )
 
         all_groups, group_0_heads, group_1_heads = range(GROUPS), range(REP), range(REP, HEADS)
-        unit_heads, round_heads, all_queries = range(2), range(REP), range(P)
+        unit_heads, round_heads = range(2), range(REP)
         first_kT_ps = side_bank.tile([P, GROUPS, TILES, P], BF16, tag="side")
         first_qT_ps = o_bank.tile([P, HEADS, P], BF16, tag="o")
         transpose_keys(0, first_kT_ps, range(1))
         keep_keys(0, first_kT_ps, range(1), nc.vector.tensor_copy)
         transpose_queries(0, first_qT_ps, range(REP))
         keep_queries(0, first_qT_ps, range(REP), nc.scalar.copy)
-        for a in range(2):
-            score_tile(0, a)
-            negate_maxima(0, a)
         transpose_keys(0, first_kT_ps, range(1, GROUPS))
         keep_keys(0, first_kT_ps, range(1, GROUPS), nc.vector.tensor_copy)
-        transpose_queries(0, first_qT_ps, range(REP, HEADS))
-        keep_queries(0, first_qT_ps, range(REP, HEADS), nc.vector.tensor_copy)
-        for a in range(2):
-            score_tile(1, a)
-            negate_maxima(1, a)
+        for n in range(2):
+            for a in range(2):
+                score_tile(n, a)
+                negate_maxima(n, a)
+            if n == 0:
+                transpose_queries(0, first_qT_ps, range(REP, HEADS))
+                keep_queries(0, first_qT_ps, range(REP, HEADS), nc.scalar.copy)
 
         side_ps = None
         wo_ps = None
@@ -405,11 +410,9 @@ def tile_attention_pb_t_kernel(tc, q_rot, k_rot, v, wo, out):
             if n % 2 == 1 and 7 <= n:
                 o_ps = o_bank.tile([P, REP * P], F32, tag="o")
                 multiply_by_v((n - 7) // 2, o_ps, round_heads)
-            if 7 <= n:
-                h = (n - 7) % 2
-                normalise((n - 7) // 2, range(h * P // 2, (h + 1) * P // 2))
-            if 2 <= n:
-                quantise_e((n - 2) // 2, range(n % 2 * 2, n % 2 * 2 + 2))
+                normalise((n - 7) // 2)
+            if n % 2 == 0 and 2 <= n:
+                quantise_e((n - 2) // 2, round_heads)
             if phase == 2 and 0 <= t - 2:
                 quantise_o(t - 2, all_groups)
             if phase == 0 and t % TILES == 0 and t > 0:
@@ -443,43 +446,41 @@ def tile_attention_pb_t_kernel(tc, q_rot, k_rot, v, wo, out):
         exponential(n - 1, 1)
         group_e(n - 2, unit_heads, nc.scalar.copy)
         transpose_e(n - 1, 1)
-        normalise(r - 4, range(P // 2, P))
+        o_ps = o_bank.tile([P, REP * P], F32, tag="o")
+        multiply_by_v(r - 3, o_ps, round_heads)
         quantise_o(t - 2, all_groups)
-        side_ps = side_bank.tile([P, MODEL], F32, tag="side")
-        project(t - 2, side_ps, all_groups)
         keep_factors(r - 1, factors_ps, nc.vector.tensor_copy)
         quantise_e(r - 1, round_heads)
-        store(t - 2, side_ps, [nc.vector.tensor_copy])
 
         exponential(n, 0)
         transpose_e(n, 0)
         exponential(n, 1)
-        group_e(n - 1, unit_heads, nc.scalar.copy)
-        o_ps = o_bank.tile([P, REP * P], F32, tag="o")
-        multiply_by_v(r - 3, o_ps, round_heads)
-        normalise(r - 3, all_queries)
-        o_ps = score_banks.tile([P, REP * P], F32, tag="scores")
-        multiply_by_v(r - 2, o_ps, round_heads)
         transpose_e(n, 1)
+        side_ps = side_bank.tile([P, MODEL], F32, tag="side")
+        project(t - 2, side_ps, all_groups)
+        group_e(n - 1, unit_heads, nc.scalar.copy)
         group_e(n, unit_heads, nc.scalar.copy)
-        o_ps = score_banks.tile([P, REP * P], F32, tag="scores")
-        multiply_by_v(r - 1, o_ps, round_heads)
+        quantise_e(r, range(2))
         factors_ps = turn_factors(r)
         keep_factors(r, factors_ps, nc.scalar.copy)
-        quantise_e(r, range(2))
-        normalise(r - 2, all_queries)
-        o_ps = score_banks.tile([P, REP * P], F32, tag="scores")
-        multiply_by_v(r, o_ps, range(2))
         quantise_e(r, range(2, REP))
-        multiply_by_v(r, o_ps, range(2, REP))
-        normalise(r - 1, all_queries)
+        normalise(r - 3)
+        o_ps = score_banks.tile([P, REP * P], F32, tag="scores")
+        multiply_by_v(r - 2, o_ps, round_heads)
+        normalise(r - 2)
+        o_ps = score_banks.tile([P, REP * P], F32, tag="scores")
+        multiply_by_v(r - 1, o_ps, round_heads)
+        store(t - 2, side_ps, [nc.scalar.copy])
+        o_ps = score_banks.tile([P, REP * P], F32, tag="scores")
+        multiply_by_v(r, o_ps, round_heads)
+        normalise(r - 1)
         quantise_o(t - 1, all_groups)
-        normalise(r, all_queries)
+        normalise(r)
         side_ps = side_bank.tile([P, MODEL], F32, tag="side")
         project(t - 1, side_ps, all_groups)
         store(t - 1, side_ps, [nc.scalar.copy])
         quantise_o(t, range(1))
         quantise_o(t, range(1, GROUPS))
-        side_ps = side_bank.tile([P, MODEL], F32, tag="side")
-        project(t, side_ps, all_groups)
-        store(t, side_ps, [nc.vector.tensor_copy, nc.scalar.copy])
+        out_ps = score_banks.tile([P, MODEL], F32, tag="scores")
+        project(t, out_ps, all_groups)
+        store(t, out_ps, [nc.vector.tensor_copy, nc.scalar.copy])

@@ -392,11 +392,10 @@ def tile_attention_pb_t_kernel(tc, q_rot, k_rot, v, wo, out):
                 score_tile(n + 2, a)
                 negate_maxima(n + 2, a)
                 transpose_e(n, a)
-                b, piece = (t + 1) // TILES, phase * 2 + a
                 if n < UNITS_PER_TILE:
-                    group_values(0, piece)
-                elif (t + 1) % TILES == 0 and b < BATCH:
-                    group_values(b, piece)
+                    group_values(0, phase * 2 + a)
+                elif a == 0 and t % TILES >= TILES // 2 and t // TILES + 1 < BATCH:
+                    group_values(t // TILES + 1, n % VALUE_PIECES)
 
             if 1 <= n:
                 group_e(n - 1, unit_heads, nc.scalar.copy)

@@ -42,8 +42,8 @@ def tile_attention_pb_t_kernel(tc, q_rot, k_rot, v, wo, out):
         constants = ctx.enter_context(tc.tile_pool(name="constants", bufs=1))
         resident = ctx.enter_context(tc.tile_pool(name="resident", bufs=1))
         per_batch = ctx.enter_context(tc.tile_pool(name="per_batch", bufs=2))
-        per_tile = ctx.enter_context(tc.tile_pool(name="per_tile", bufs=3))
-        per_unit = ctx.enter_context(tc.tile_pool(name="per_unit", bufs=5))
+        per_tile = ctx.enter_context(tc.tile_pool(name="per_tile", bufs=4))
+        per_unit = ctx.enter_context(tc.tile_pool(name="per_unit", bufs=7))
         results = ctx.enter_context(tc.tile_pool(name="results", bufs=8))
         score_banks = ctx.enter_context(tc.psum_pool(name="score_banks", bufs=4))
         eT_banks = ctx.enter_context(tc.psum_pool(name="eT_banks", bufs=2))
@@ -378,14 +378,13 @@ def tile_attention_pb_t_kernel(tc, q_rot, k_rot, v, wo, out):
             if phase == 1 and t // TILES + 1 < BATCH:
                 if t % TILES == 0:
                     load_keys(t // TILES + 1)
-                load_queries(t // TILES + 1, t % TILES)
-                if t % TILES == 1:
                     load_values(t // TILES + 1)
+                load_queries(t // TILES + 1, t % TILES)
 
             if phase == 0 and 0 <= t - 1:
                 spread_factors(t - 1)
-            if phase == 0 and 0 <= t - 3:
-                store(t - 3, side_ps, [nc.vector.tensor_copy])
+            if phase == 0 and 0 <= t - 4:
+                store(t - 4, side_ps, [nc.vector.tensor_copy])
 
             for a in range(2):
                 exponential(n, a)
@@ -406,14 +405,14 @@ def tile_attention_pb_t_kernel(tc, q_rot, k_rot, v, wo, out):
             if phase == 3 and new_batch:
                 keep_keys((t + 2) // TILES, side_ps, all_groups, nc.scalar.copy)
 
-            if n % 2 == 1 and 7 <= n:
+            if n % 2 == 1 and 11 <= n:
                 o_ps = o_bank.tile([P, REP * P], F32, tag="o")
-                multiply_by_v((n - 7) // 2, o_ps, round_heads)
-                normalise((n - 7) // 2)
+                multiply_by_v((n - 11) // 2, o_ps, round_heads)
+                normalise((n - 11) // 2)
             if n % 2 == 0 and 2 <= n:
                 quantise_e((n - 2) // 2, round_heads)
-            if phase == 2 and 0 <= t - 2:
-                quantise_o(t - 2, all_groups)
+            if phase == 2 and 0 <= t - 3:
+                quantise_o(t - 3, all_groups)
             if phase == 0 and t % TILES == 0 and t > 0:
                 quantise_values(t // TILES)
             if n in (1, 3):
@@ -434,9 +433,9 @@ def tile_attention_pb_t_kernel(tc, q_rot, k_rot, v, wo, out):
             if phase == 2 and new_batch:
                 side_ps = side_bank.tile([P, GROUPS, TILES, P], BF16, tag="side")
                 transpose_keys((t + 2) // TILES, side_ps, all_groups)
-            if phase == 3 and 0 <= t - 2:
+            if phase == 3 and 0 <= t - 3:
                 side_ps = side_bank.tile([P, MODEL], F32, tag="side")
-                project(t - 2, side_ps, all_groups)
+                project(t - 3, side_ps, all_groups)
 
         n, t, r = n_units - 1, n_tiles - 1, n_tiles * GROUPS - 1
         exponential(n - 1, 0)
@@ -446,24 +445,34 @@ def tile_attention_pb_t_kernel(tc, q_rot, k_rot, v, wo, out):
         group_e(n - 2, unit_heads, nc.scalar.copy)
         transpose_e(n - 1, 1)
         o_ps = o_bank.tile([P, REP * P], F32, tag="o")
-        multiply_by_v(r - 3, o_ps, round_heads)
-        quantise_o(t - 2, all_groups)
-        keep_factors(r - 1, factors_ps, nc.vector.tensor_copy)
+        multiply_by_v(r - 5, o_ps, round_heads)
+        quantise_o(t - 3, all_groups)
+        normalise(r - 5)
+        side_ps = side_bank.tile([P, MODEL], F32, tag="side")
+        project(t - 3, side_ps, all_groups)
         quantise_e(r - 1, round_heads)
 
         exponential(n, 0)
+        o_ps = o_bank.tile([P, REP * P], F32, tag="o")
+        multiply_by_v(r - 4, o_ps, round_heads)
         transpose_e(n, 0)
         exponential(n, 1)
+        normalise(r - 4)
         transpose_e(n, 1)
-        side_ps = side_bank.tile([P, MODEL], F32, tag="side")
-        project(t - 2, side_ps, all_groups)
+        o_ps = o_bank.tile([P, REP * P], F32, tag="o")
+        multiply_by_v(r - 3, o_ps, round_heads)
+        keep_factors(r - 1, factors_ps, nc.vector.tensor_copy)
+        quantise_o(t - 2, all_groups)
         group_e(n - 1, unit_heads, nc.scalar.copy)
+        store(t - 3, side_ps, [nc.scalar.copy])
         group_e(n, unit_heads, nc.scalar.copy)
+        normalise(r - 3)
         quantise_e(r, range(2))
         factors_ps = turn_factors(r)
         keep_factors(r, factors_ps, nc.scalar.copy)
         quantise_e(r, range(2, REP))
-        normalise(r - 3)
+        side_ps = side_bank.tile([P, MODEL], F32, tag="side")
+        project(t - 2, side_ps, all_groups)
         o_ps = score_banks.tile([P, REP * P], F32, tag="scores")
         multiply_by_v(r - 2, o_ps, round_heads)
         normalise(r - 2)

@@ -409,6 +409,8 @@ def tile_attention_pb_t_kernel(tc, q_rot, k_rot, v, wo, out):
                 o_ps = o_bank.tile([P, REP * P], F32, tag="o")
                 multiply_by_v((n - 11) // 2, o_ps, round_heads)
                 normalise((n - 11) // 2)
+            if n % 2 == 0 and 8 <= n:
+                multiply_by_v(max((n - 12) // 2, 0), o_bank.tile([P, REP * P], F32, name="unread", tag="o"), round_heads)
             if n % 2 == 0 and 2 <= n:
                 quantise_e((n - 2) // 2, round_heads)
             if phase == 2 and 0 <= t - 3:

@@ -216,7 +216,7 @@ def tile_attention_pb_t_kernel(tc, q_rot, k_rot, v, wo, out):
 
         def transpose_e(n, a):
             if a == 0:
-                eT_ps = eT_banks.tile([P, 2, 2, P], F32)
+                eT_ps = eT_banks.tile([P, 2, 2, P], F32, tag="eT")
                 eT_of[n] = eT_ps
             e_words = e_sb_of[n][:].bitcast(F32)
             for u in range(2):
@@ -246,9 +246,9 @@ def tile_attention_pb_t_kernel(tc, q_rot, k_rot, v, wo, out):
                 in_=e_grouped_of[r][:, heads.start : heads.stop, :, :].rearrange("p i q u -> p (i q u)").bitcast(BF16),
             )
 
-        def spread_factors(t):
+        def spread_factors(t, sums):
             inv_sum = per_tile.tile([P, HEADS], F32)
-            nc.vector.reciprocal(out=inv_sum[:], in_=row_sum_of[t][:])
+            nc.vector.reciprocal(out=inv_sum[:].rearrange("q (g i) -> q g i", g=GROUPS), in_=sums)
             park = out_rows(t, PARK_ROWS).rearrange("r m -> (r m)")
             nc.sync.dma_start(out=park.rearrange("(q h) -> q h", h=HEADS), in_=inv_sum[:])
             factors = per_tile.tile([P, P * HEADS], F32)
@@ -256,11 +256,14 @@ def tile_attention_pb_t_kernel(tc, q_rot, k_rot, v, wo, out):
             for g in range(GROUPS):
                 factors_of[2 * t + g] = factors[:].rearrange("d (q h) -> d q h", h=HEADS)[:, :, g * REP : (g + 1) * REP]
 
-        def turn_factors(r):
-            inv_sum = per_tile.tile([P, REP], F32)
+        def invert_sums(r):
+            inv_sum = per_tile.tile([P, REP], F32, name="round_inv_sum")
             group = slice((r % GROUPS) * REP, (r % GROUPS + 1) * REP)
             nc.vector.reciprocal(out=inv_sum[:], in_=row_sum_of[r // GROUPS][:, group])
-            factors_ps = score_banks.tile([P, REP, P], F32, tag="scores")
+            return inv_sum
+
+        def turn_factors(inv_sum, bank, tag):
+            factors_ps = bank.tile([P, REP, P], F32, tag=tag)
             for i in range(REP):
                 nc.tensor.transpose(factors_ps[:, i, :], inv_sum[:, i : i + 1].to_broadcast([P, P]), identity_f32[:])
             return factors_ps
@@ -370,6 +373,7 @@ def tile_attention_pb_t_kernel(tc, q_rot, k_rot, v, wo, out):
 
         side_ps = None
         wo_ps = None
+        hurry = n_units - 6
         for n in range(n_units - 2):
             phase = n % UNITS_PER_TILE
             t = n // UNITS_PER_TILE
@@ -381,8 +385,10 @@ def tile_attention_pb_t_kernel(tc, q_rot, k_rot, v, wo, out):
                     load_values(t // TILES + 1)
                 load_queries(t // TILES + 1, t % TILES)
 
-            if phase == 0 and 0 <= t - 1:
-                spread_factors(t - 1)
+            if phase == 0 and 0 <= t - 1 and n < hurry:
+                spread_factors(t - 1, row_sum_of[t - 1][:].rearrange("q (g i) -> q g i", g=GROUPS))
+            if n == hurry:
+                spread_factors(t, row_sum_of[t][:, :REP].unsqueeze(1).to_broadcast([P, GROUPS, REP]))
             if phase == 0 and 0 <= t - 4:
                 store(t - 4, side_ps, [nc.vector.tensor_copy])
 
@@ -393,8 +399,10 @@ def tile_attention_pb_t_kernel(tc, q_rot, k_rot, v, wo, out):
                 transpose_e(n, a)
                 if n < UNITS_PER_TILE:
                     group_values(0, phase * 2 + a)
-                elif a == 0 and t % TILES >= TILES // 2 and t // TILES + 1 < BATCH:
-                    group_values(t // TILES + 1, n % VALUE_PIECES)
+
+            if n % 2 == 1 and t % TILES >= TILES // 2 and t // TILES + 1 < BATCH:
+                group_values(t // TILES + 1, n % VALUE_PIECES - 1)
+                group_values(t // TILES + 1, n % VALUE_PIECES)
 
             if 1 <= n:
                 group_e(n - 1, unit_heads, nc.scalar.copy)
@@ -405,11 +413,12 @@ def tile_attention_pb_t_kernel(tc, q_rot, k_rot, v, wo, out):
             if phase == 3 and new_batch:
                 keep_keys((t + 2) // TILES, side_ps, all_groups, nc.scalar.copy)
 
-            if n % 2 == 1 and 11 <= n:
+            if n % 2 == 1 and 11 <= n or hurry <= n:
+                divided = (n - 11) // 2 if n < hurry else (hurry - 10) // 2 + n - hurry
                 o_ps = o_bank.tile([P, REP * P], F32, tag="o")
-                multiply_by_v((n - 11) // 2, o_ps, round_heads)
-                normalise((n - 11) // 2)
-            if n % 2 == 0 and 8 <= n:
+                multiply_by_v(divided, o_ps, round_heads)
+                normalise(divided)
+            if n % 2 == 0 and 8 <= n < hurry:
                 multiply_by_v(max((n - 12) // 2, 0), o_bank.tile([P, REP * P], F32, name="unread", tag="o"), round_heads)
             if n % 2 == 0 and 2 <= n:
                 quantise_e((n - 2) // 2, round_heads)
@@ -440,57 +449,55 @@ def tile_attention_pb_t_kernel(tc, q_rot, k_rot, v, wo, out):
                 project(t - 3, side_ps, all_groups)
 
         n, t, r = n_units - 1, n_tiles - 1, n_tiles * GROUPS - 1
+
+        def result_bank(r, bank, tag):
+            o_ps = bank.tile([P, REP * P], F32, tag=tag)
+            multiply_by_v(r, o_ps, round_heads)
+
         exponential(n - 1, 0)
-        factors_ps = turn_factors(r - 1)
         transpose_e(n - 1, 0)
         exponential(n - 1, 1)
-        group_e(n - 2, unit_heads, nc.scalar.copy)
+        inv_1, inv_2 = invert_sums(r - 1), invert_sums(r - 2)
         transpose_e(n - 1, 1)
-        o_ps = o_bank.tile([P, REP * P], F32, tag="o")
-        multiply_by_v(r - 5, o_ps, round_heads)
-        quantise_o(t - 3, all_groups)
-        normalise(r - 5)
-        side_ps = side_bank.tile([P, MODEL], F32, tag="side")
-        project(t - 3, side_ps, all_groups)
-        quantise_e(r - 1, round_heads)
-
+        group_e(n - 2, unit_heads, nc.scalar.copy)
+        result_bank(r - 3, o_bank, "o")
         exponential(n, 0)
-        o_ps = o_bank.tile([P, REP * P], F32, tag="o")
-        multiply_by_v(r - 4, o_ps, round_heads)
         transpose_e(n, 0)
+        factors_1 = turn_factors(inv_1, score_banks, "scores")
         exponential(n, 1)
-        normalise(r - 4)
         transpose_e(n, 1)
-        o_ps = o_bank.tile([P, REP * P], F32, tag="o")
-        multiply_by_v(r - 3, o_ps, round_heads)
-        keep_factors(r - 1, factors_ps, nc.vector.tensor_copy)
-        quantise_o(t - 2, all_groups)
-        group_e(n - 1, unit_heads, nc.scalar.copy)
-        store(t - 3, side_ps, [nc.scalar.copy])
-        group_e(n, unit_heads, nc.scalar.copy)
+        factors_2 = turn_factors(inv_2, score_banks, "scores")
+        quantise_o(t - 3, all_groups)
+        quantise_e(r - 1, round_heads)
         normalise(r - 3)
+        quantise_o(t - 2, all_groups)
+        result_bank(r - 1, score_banks, "scores")
+        group_e(n - 1, unit_heads, nc.scalar.copy)
+        group_e(n, unit_heads, nc.scalar.copy)
+        keep_factors(r - 1, factors_1, nc.scalar.copy)
+        inv_0 = invert_sums(r)
         quantise_e(r, range(2))
-        factors_ps = turn_factors(r)
-        keep_factors(r, factors_ps, nc.scalar.copy)
         quantise_e(r, range(2, REP))
-        side_ps = side_bank.tile([P, MODEL], F32, tag="side")
-        project(t - 2, side_ps, all_groups)
-        o_ps = score_banks.tile([P, REP * P], F32, tag="scores")
-        multiply_by_v(r - 2, o_ps, round_heads)
-        normalise(r - 2)
-        o_ps = score_banks.tile([P, REP * P], F32, tag="scores")
-        multiply_by_v(r - 1, o_ps, round_heads)
-        store(t - 2, side_ps, [nc.scalar.copy])
-        o_ps = score_banks.tile([P, REP * P], F32, tag="scores")
-        multiply_by_v(r, o_ps, round_heads)
+        factors_0 = turn_factors(inv_0, eT_banks, "eT")
+        result_bank(r - 2, o_bank, "o")
         normalise(r - 1)
+        keep_factors(r - 2, factors_2, nc.scalar.copy)
+        keep_factors(r, factors_0, nc.scalar.copy)
+        result_bank(r, score_banks, "scores")
+        normalise(r - 2)
+        quantise_o(t, range(1))
         quantise_o(t - 1, all_groups)
         normalise(r)
         side_ps = side_bank.tile([P, MODEL], F32, tag="side")
-        project(t - 1, side_ps, all_groups)
-        store(t - 1, side_ps, [nc.scalar.copy])
-        quantise_o(t, range(1))
+        project(t - 3, side_ps, all_groups)
+        store(t - 3, side_ps, [nc.scalar.copy])
+        out_ps = o_bank.tile([P, MODEL], F32, tag="o")
+        project(t - 2, out_ps, all_groups)
+        store(t - 2, out_ps, [nc.scalar.copy])
         quantise_o(t, range(1, GROUPS))
+        side_ps = side_bank.tile([P, MODEL], F32, tag="side")
+        project(t - 1, side_ps, all_groups)
         out_ps = score_banks.tile([P, MODEL], F32, tag="scores")
         project(t, out_ps, all_groups)
+        store(t - 1, side_ps, [nc.scalar.copy])
         store(t, out_ps, [nc.vector.tensor_copy, nc.scalar.copy])

@@ -28,7 +28,7 @@ SCALE = HEAD_DIM ** -0.5
 UNITS_PER_TILE = 4
 VALUE_PIECES = 8
 WARM_UP = 5
-PARK_ROWS = P * HEADS // MODEL
+WORDS = 2
 
 FLOPS = 2 * BATCH * HEADS * POSITIONS * POSITIONS * HEAD_DIM * 2 + 2 * BATCH * POSITIONS * FEATURES * MODEL
 
@@ -43,7 +43,7 @@ def tile_attention_pb_t_kernel(tc, q_rot, k_rot, v, wo, out):
         resident = ctx.enter_context(tc.tile_pool(name="resident", bufs=1))
         per_batch = ctx.enter_context(tc.tile_pool(name="per_batch", bufs=2))
         per_tile = ctx.enter_context(tc.tile_pool(name="per_tile", bufs=4))
-        per_unit = ctx.enter_context(tc.tile_pool(name="per_unit", bufs=7))
+        per_unit = ctx.enter_context(tc.tile_pool(name="per_unit", bufs=5))
         results = ctx.enter_context(tc.tile_pool(name="results", bufs=8))
         score_banks = ctx.enter_context(tc.psum_pool(name="score_banks", bufs=4))
         eT_banks = ctx.enter_context(tc.psum_pool(name="eT_banks", bufs=2))
@@ -110,7 +110,7 @@ def tile_attention_pb_t_kernel(tc, q_rot, k_rot, v, wo, out):
 
         kT_of, v_grouped_of, v_codes_of, v_scales_of = {}, {}, {}, {}
         qT_of, o_grouped_of, o_codes_of, o_scales_of = {}, {}, {}, {}
-        row_sum_of, factors_of, o_ps_of = {}, {}, {}
+        row_sum_of, inv_sum_of, o_ps_of, o_sb_of = {}, {}, {}, {}
         row_max_of, neg_max_of, scores_of, e_sb_of, eT_of, e_grouped_of, e_codes_of, e_scales_of = (
             {}, {}, {}, {}, {}, {}, {}, {},
         )
@@ -216,16 +216,16 @@ def tile_attention_pb_t_kernel(tc, q_rot, k_rot, v, wo, out):
 
         def transpose_e(n, a):
             if a == 0:
-                eT_ps = eT_banks.tile([P, 2, 2, P], F32, tag="eT")
+                eT_ps = eT_banks.tile([P, 2, WORDS, P], F32)
                 eT_of[n] = eT_ps
             e_words = e_sb_of[n][:].bitcast(F32)
-            for u in range(2):
-                first = (2 * a + u) * P
+            for u in range(WORDS):
+                first = (WORDS * a + u) * P
                 nc.tensor.transpose(eT_of[n][:, a, u, :], e_words[:, first : first + P], identity_f32[:])
 
         def group_e(n, heads, copy):
             if n % 2 == 0 and heads.start == 0:
-                e_grouped = per_unit.tile([P, REP, P, 2], F32, align_bytes=64)
+                e_grouped = per_unit.tile([P, REP, P, WORDS], F32, align_bytes=64)
                 e_grouped_of[n // 2] = e_grouped
             first = (n % 2) * 2
             copy(
@@ -246,60 +246,50 @@ def tile_attention_pb_t_kernel(tc, q_rot, k_rot, v, wo, out):
                 in_=e_grouped_of[r][:, heads.start : heads.stop, :, :].rearrange("p i q u -> p (i q u)").bitcast(BF16),
             )
 
-        def spread_factors(t, sums):
-            inv_sum = per_tile.tile([P, HEADS], F32)
-            nc.vector.reciprocal(out=inv_sum[:].rearrange("q (g i) -> q g i", g=GROUPS), in_=sums)
-            park = out_rows(t, PARK_ROWS).rearrange("r m -> (r m)")
-            nc.sync.dma_start(out=park.rearrange("(q h) -> q h", h=HEADS), in_=inv_sum[:])
-            factors = per_tile.tile([P, P * HEADS], F32)
-            nc.sync.dma_start(out=factors[:], in_=park.partition_broadcast(P))
-            for g in range(GROUPS):
-                factors_of[2 * t + g] = factors[:].rearrange("d (q h) -> d q h", h=HEADS)[:, :, g * REP : (g + 1) * REP]
+        def invert_sums(t, groups):
+            if groups.start == 0:
+                inv_sum = per_tile.tile([P, HEADS], F32)
+                inv_sum_of[t] = inv_sum
+            some = slice(groups.start * REP, groups.stop * REP)
+            nc.vector.reciprocal(out=inv_sum_of[t][:, some], in_=row_sum_of[t][:, some])
 
-        def invert_sums(r):
-            inv_sum = per_tile.tile([P, REP], F32, name="round_inv_sum")
-            group = slice((r % GROUPS) * REP, (r % GROUPS + 1) * REP)
-            nc.vector.reciprocal(out=inv_sum[:], in_=row_sum_of[r // GROUPS][:, group])
-            return inv_sum
-
-        def turn_factors(inv_sum, bank, tag):
-            factors_ps = bank.tile([P, REP, P], F32, tag=tag)
-            for i in range(REP):
-                nc.tensor.transpose(factors_ps[:, i, :], inv_sum[:, i : i + 1].to_broadcast([P, P]), identity_f32[:])
-            return factors_ps
-
-        def keep_factors(r, factors_ps, copy):
-            round_factors = per_tile.tile([P, REP, P], F32)
-            copy(out=round_factors[:], in_=factors_ps[:])
-            factors_of[r] = round_factors[:].rearrange("d i q -> d q i")
-
-        def multiply_by_v(r, o_ps, heads):
+        def multiply_by_v(r, o_ps):
             b = r // (TILES * GROUPS)
             g_cols = slice((r % GROUPS) * HEAD_DIM, (r % GROUPS + 1) * HEAD_DIM)
-            q_cols = slice(heads.start * P, heads.stop * P)
-            nc.tensor.matmul_mx(
-                out=o_ps[:, q_cols],
-                lhsT=v_codes_of[b][:, g_cols].bitcast(FP8X4),
-                lhsT_scale=v_scales_of[b][:, g_cols],
-                rhs=e_codes_of[r][:, q_cols].bitcast(FP8X4),
-                rhs_scale=e_scales_of[r][:, q_cols],
-                start=True,
-                stop=True,
-            )
+            for i in range(REP):
+                q_cols = slice(i * P, (i + 1) * P)
+                nc.tensor.matmul_mx(
+                    out=o_ps[:, i, :],
+                    lhsT=e_codes_of[r][:, q_cols].bitcast(FP8X4),
+                    lhsT_scale=e_scales_of[r][:, q_cols],
+                    rhs=v_codes_of[b][:, g_cols].bitcast(FP8X4),
+                    rhs_scale=v_scales_of[b][:, g_cols],
+                    start=True,
+                    stop=True,
+                )
             o_ps_of[r] = o_ps
 
         def normalise(r):
             t = r // GROUPS
             g = r % GROUPS
             if g == 0:
-                o_grouped = per_tile.tile([P, GROUPS, P, PACK], BF16, align_bytes=64)
+                o_sb = per_tile.tile([P, GROUPS, REP, HEAD_DIM], BF16)
+                o_sb_of[t] = o_sb
+            factors = inv_sum_of[t][:, g * REP : (g + 1) * REP].unsqueeze(2).to_broadcast([P, REP, HEAD_DIM])
+            nc.vector.tensor_tensor(out=o_sb_of[t][:, g, :, :], in0=o_ps_of[r][:], in1=factors, op=MULT)
+
+        def transpose_o(t, oT_ps, groups):
+            for g in groups:
+                o_words = o_sb_of[t][:, g, :, :].rearrange("q i d -> q (i d)").bitcast(F32)
+                for u in range(WORDS):
+                    nc.tensor.transpose(oT_ps[:, g, u, :], o_words[:, u * P : (u + 1) * P], identity_f32[:])
+
+        def group_o(t, oT_ps, groups, copy):
+            if groups.start == 0:
+                o_grouped = per_tile.tile([P, GROUPS, P, WORDS], F32, align_bytes=64)
                 o_grouped_of[t] = o_grouped
-            nc.vector.tensor_tensor(
-                out=o_grouped_of[t][:, g, :, :],
-                in0=o_ps_of[r][:].rearrange("d (i q) -> d q i", i=REP),
-                in1=factors_of[r],
-                op=MULT,
-            )
+            some = slice(groups.start, groups.stop)
+            copy(out=o_grouped_of[t][:, some, :, :], in_=oT_ps[:, some, :, :].rearrange("d g u q -> d g q u"))
 
         def quantise_o(t, groups):
             if groups.start == 0:
@@ -311,7 +301,7 @@ def tile_attention_pb_t_kernel(tc, q_rot, k_rot, v, wo, out):
             nc.vector.quantize_mx(
                 out=o_codes_of[t][:, cols].bitcast(FP8X4),
                 scales=o_scales_of[t][:, cols],
-                in_=o_grouped_of[t][:, groups.start : groups.stop, :, :].rearrange("d g q i -> d (g q i)"),
+                in_=o_grouped_of[t][:, groups.start : groups.stop, :, :].rearrange("d g q u -> d (g q u)").bitcast(BF16),
             )
 
         def project(t, out_ps, groups):
@@ -333,27 +323,30 @@ def tile_attention_pb_t_kernel(tc, q_rot, k_rot, v, wo, out):
                 copy(out=out_sb[:, c * width : (c + 1) * width], in_=out_ps[:, c * width : (c + 1) * width])
             nc.sync.dma_start(out=out_rows(t, P), in_=out_sb[:])
 
-        wo_grouped = constants.tile([P, GROUPS, MODEL, PACK], BF16, align_bytes=64)
+        wo_grouped = constants.tile([P, GROUPS, MODEL, WORDS], F32, align_bytes=64)
         wo_codes = constants.tile([P, GROUPS * MODEL], U32, align_bytes=64)
         wo_scales = constants.tile([P, GROUPS * MODEL], U8, align_bytes=64)
 
         def transpose_wo(g):
-            wo_ps = o_bank.tile([P, REP, 2, P], BF16, tag="o")
-            for i in range(REP):
+            wo_ps = o_bank.tile([P, WORDS, 2, P], F32, tag="o")
+            wo_words = wo_sb[:].bitcast(F32)
+            for u in range(WORDS):
                 for a in range(2):
-                    first = a * FEATURES + (g * REP + i) * HEAD_DIM
-                    nc.tensor.transpose(wo_ps[:, i, a, :], wo_sb[:, first : first + HEAD_DIM], identity_bf16[:])
+                    first = (a * FEATURES + g * REP * HEAD_DIM) // 2 + u * P
+                    nc.tensor.transpose(wo_ps[:, u, a, :], wo_words[:, first : first + P], identity_f32[:])
             return wo_ps
 
         def group_wo(g, wo_ps):
-            nc.vector.tensor_copy(out=wo_grouped[:, g, :, :], in_=wo_ps[:].rearrange("d i a m -> d (a m) i"))
+            nc.vector.tensor_copy(out=wo_grouped[:, g, :, :], in_=wo_ps[:].rearrange("d u a m -> d (a m) u"))
 
         def quantise_wo():
             nc.vector.quantize_mx(
-                out=wo_codes[:].bitcast(FP8X4), scales=wo_scales[:], in_=wo_grouped[:].rearrange("d g m i -> d (g m i)")
+                out=wo_codes[:].bitcast(FP8X4),
+                scales=wo_scales[:],
+                in_=wo_grouped[:].rearrange("d g m u -> d (g m u)").bitcast(BF16),
             )
 
-        all_groups, group_0_heads, group_1_heads = range(GROUPS), range(REP), range(REP, HEADS)
+        all_groups, all_heads = range(GROUPS), range(HEADS)
         unit_heads, round_heads = range(2), range(REP)
         first_kT_ps = side_bank.tile([P, GROUPS, TILES, P], BF16, tag="side")
         first_qT_ps = o_bank.tile([P, HEADS, P], BF16, tag="o")
@@ -373,7 +366,6 @@ def tile_attention_pb_t_kernel(tc, q_rot, k_rot, v, wo, out):
 
         side_ps = None
         wo_ps = None
-        hurry = n_units - 6
         for n in range(n_units - 2):
             phase = n % UNITS_PER_TILE
             t = n // UNITS_PER_TILE
@@ -385,12 +377,12 @@ def tile_attention_pb_t_kernel(tc, q_rot, k_rot, v, wo, out):
                     load_values(t // TILES + 1)
                 load_queries(t // TILES + 1, t % TILES)
 
-            if phase == 0 and 0 <= t - 1 and n < hurry:
-                spread_factors(t - 1, row_sum_of[t - 1][:].rearrange("q (g i) -> q g i", g=GROUPS))
-            if n == hurry:
-                spread_factors(t, row_sum_of[t][:, :REP].unsqueeze(1).to_broadcast([P, GROUPS, REP]))
-            if phase == 0 and 0 <= t - 4:
-                store(t - 4, side_ps, [nc.vector.tensor_copy])
+            if phase == 1 and 0 <= t - 2:
+                group_o(t - 2, side_ps, all_groups, nc.vector.tensor_copy)
+            if phase == 0 and 0 <= t - 1:
+                invert_sums(t - 1, all_groups)
+            if phase == 2 and 0 <= t - 2:
+                quantise_o(t - 2, all_groups)
 
             for a in range(2):
                 exponential(n, a)
@@ -406,98 +398,91 @@ def tile_attention_pb_t_kernel(tc, q_rot, k_rot, v, wo, out):
 
             if 1 <= n:
                 group_e(n - 1, unit_heads, nc.scalar.copy)
-            if phase == 1 and t + 1 < n_tiles:
-                keep_queries(t + 1, side_ps, group_0_heads, nc.scalar.copy)
-            if phase == 2 and t + 1 < n_tiles:
-                keep_queries(t + 1, side_ps, group_1_heads, nc.scalar.copy)
-            if phase == 3 and new_batch:
+            if (phase == 0 and 1 <= t or n == 1) and t + 1 < n_tiles:
+                keep_queries(t + 1, side_ps, all_heads, nc.scalar.copy)
+            if phase == 2 and new_batch:
                 keep_keys((t + 2) // TILES, side_ps, all_groups, nc.scalar.copy)
+            if phase == 3 and 0 <= t - 2:
+                store(t - 2, side_ps, [nc.scalar.copy])
 
-            if n % 2 == 1 and 11 <= n or hurry <= n:
-                divided = (n - 11) // 2 if n < hurry else (hurry - 10) // 2 + n - hurry
-                o_ps = o_bank.tile([P, REP * P], F32, tag="o")
-                multiply_by_v(divided, o_ps, round_heads)
-                normalise(divided)
-            if n % 2 == 0 and 8 <= n < hurry:
-                multiply_by_v(max((n - 12) // 2, 0), o_bank.tile([P, REP * P], F32, name="unread", tag="o"), round_heads)
+            if n % 2 == 1 and 5 <= n:
+                o_ps = o_bank.tile([P, REP, HEAD_DIM], F32, tag="o")
+                multiply_by_v((n - 5) // 2, o_ps)
+                normalise((n - 5) // 2)
             if n % 2 == 0 and 2 <= n:
                 quantise_e((n - 2) // 2, round_heads)
-            if phase == 2 and 0 <= t - 3:
-                quantise_o(t - 3, all_groups)
             if phase == 0 and t % TILES == 0 and t > 0:
                 quantise_values(t // TILES)
-            if n in (1, 3):
+            if n in (0, 2):
                 wo_ps = transpose_wo(n // 2)
-            if n in (2, 4):
-                group_wo(n // 2 - 1, wo_ps)
-            if n == 5:
+            if n in (1, 3):
+                group_wo(n // 2, wo_ps)
+            if n == 4:
                 quantise_values(0)
             if n == 6:
                 quantise_wo()
 
-            if phase == 0 and t + 1 < n_tiles:
-                side_ps = side_bank.tile([P, HEADS, P], BF16, tag="side")
-                transpose_queries(t + 1, side_ps, group_0_heads)
-            if phase == 1 and t + 1 < n_tiles:
-                side_ps = side_bank.tile([P, HEADS, P], BF16, tag="side")
-                transpose_queries(t + 1, side_ps, group_1_heads)
-            if phase == 2 and new_batch:
+            if phase == 0 and 0 <= t - 2:
+                side_ps = side_bank.tile([P, GROUPS, WORDS, P], F32, tag="side")
+                transpose_o(t - 2, side_ps, all_groups)
+            if phase == 1 and new_batch:
                 side_ps = side_bank.tile([P, GROUPS, TILES, P], BF16, tag="side")
                 transpose_keys((t + 2) // TILES, side_ps, all_groups)
-            if phase == 3 and 0 <= t - 3:
+            if phase == 2 and 0 <= t - 2:
                 side_ps = side_bank.tile([P, MODEL], F32, tag="side")
-                project(t - 3, side_ps, all_groups)
+                project(t - 2, side_ps, all_groups)
+            if phase == 3 and t + 2 < n_tiles or n == 0:
+                side_ps = side_bank.tile([P, HEADS, P], BF16, tag="side")
+                transpose_queries(t + 2 if phase == 3 else 1, side_ps, all_heads)
 
         n, t, r = n_units - 1, n_tiles - 1, n_tiles * GROUPS - 1
 
         def result_bank(r, bank, tag):
-            o_ps = bank.tile([P, REP * P], F32, tag=tag)
-            multiply_by_v(r, o_ps, round_heads)
+            o_ps = bank.tile([P, REP, HEAD_DIM], F32, tag=tag)
+            multiply_by_v(r, o_ps)
 
         exponential(n - 1, 0)
         transpose_e(n - 1, 0)
         exponential(n - 1, 1)
-        inv_1, inv_2 = invert_sums(r - 1), invert_sums(r - 2)
         transpose_e(n - 1, 1)
         group_e(n - 2, unit_heads, nc.scalar.copy)
-        result_bank(r - 3, o_bank, "o")
+        result_bank(r - 2, o_bank, "o")
+        quantise_o(t - 2, all_groups)
+        quantise_e(r - 1, round_heads)
+        normalise(r - 2)
+        invert_sums(t, range(1))
+
         exponential(n, 0)
         transpose_e(n, 0)
-        factors_1 = turn_factors(inv_1, score_banks, "scores")
+        side_ps = side_bank.tile([P, MODEL], F32, tag="side")
+        project(t - 2, side_ps, all_groups)
         exponential(n, 1)
         transpose_e(n, 1)
-        factors_2 = turn_factors(inv_2, score_banks, "scores")
-        quantise_o(t - 3, all_groups)
-        quantise_e(r - 1, round_heads)
-        normalise(r - 3)
-        quantise_o(t - 2, all_groups)
         result_bank(r - 1, score_banks, "scores")
         group_e(n - 1, unit_heads, nc.scalar.copy)
-        group_e(n, unit_heads, nc.scalar.copy)
-        keep_factors(r - 1, factors_1, nc.scalar.copy)
-        inv_0 = invert_sums(r)
-        quantise_e(r, range(2))
-        quantise_e(r, range(2, REP))
-        factors_0 = turn_factors(inv_0, eT_banks, "eT")
-        result_bank(r - 2, o_bank, "o")
+        store(t - 2, side_ps, [nc.vector.tensor_copy])
         normalise(r - 1)
-        keep_factors(r - 2, factors_2, nc.scalar.copy)
-        keep_factors(r, factors_0, nc.scalar.copy)
+        group_e(n, unit_heads, nc.scalar.copy)
+        oT_ps = side_bank.tile([P, GROUPS, WORDS, P], F32, tag="side")
+        transpose_o(t - 1, oT_ps, all_groups)
+        group_o(t - 1, oT_ps, all_groups, nc.scalar.copy)
+        quantise_e(r, range(2))
+        invert_sums(t, range(1, GROUPS))
+        quantise_e(r, range(2, REP))
+        oT_ps = o_bank.tile([P, GROUPS, WORDS, P], F32, tag="o")
+        transpose_o(t, oT_ps, range(1))
         result_bank(r, score_banks, "scores")
-        normalise(r - 2)
-        quantise_o(t, range(1))
+        group_o(t, oT_ps, range(1), nc.scalar.copy)
         quantise_o(t - 1, all_groups)
         normalise(r)
-        side_ps = side_bank.tile([P, MODEL], F32, tag="side")
-        project(t - 3, side_ps, all_groups)
-        store(t - 3, side_ps, [nc.scalar.copy])
-        out_ps = o_bank.tile([P, MODEL], F32, tag="o")
-        project(t - 2, out_ps, all_groups)
-        store(t - 2, out_ps, [nc.scalar.copy])
+        out_ps = score_banks.tile([P, MODEL], F32, tag="scores")
+        project(t - 1, out_ps, all_groups)
+        store(t - 1, out_ps, [nc.scalar.copy])
+        quantise_o(t, range(1))
+        oT_ps = score_banks.tile([P, GROUPS, WORDS, P], F32, tag="scores")
+        transpose_o(t, oT_ps, range(1, GROUPS))
+        group_o(t, oT_ps, range(1, GROUPS), nc.vector.tensor_copy)
         quantise_o(t, range(1, GROUPS))
         side_ps = side_bank.tile([P, MODEL], F32, tag="side")
-        project(t - 1, side_ps, all_groups)
-        out_ps = score_banks.tile([P, MODEL], F32, tag="scores")
-        project(t, out_ps, all_groups)
-        store(t - 1, side_ps, [nc.scalar.copy])
-        store(t, out_ps, [nc.vector.tensor_copy, nc.scalar.copy])
+        project(t, side_ps, all_groups)
+        store(t, side_ps, [nc.vector.tensor_copy, nc.scalar.copy])

@@ -66,10 +66,11 @@ def tile_attention_pb_t_kernel(tc, q_rot, k_rot, v, wo, out):
                 in_=k_rot[b].rearrange("s k g d -> (s k) (g d)").rearrange("(t p) f -> p t f", p=P),
             )
 
-        def load_queries(b, j):
+        def load_queries(b, j, heads):
+            cols = slice(heads.start * HEAD_DIM, heads.stop * HEAD_DIM)
             nc.sync.dma_start(
-                out=q_sb[b][:, j, :],
-                in_=q_rot[b].rearrange("s k h d -> (s k) (h d)")[j * P : (j + 1) * P, :],
+                out=q_sb[b][:, j, cols],
+                in_=q_rot[b].rearrange("s k h d -> (s k) (h d)")[j * P : (j + 1) * P, cols],
             )
 
         def load_values(b):
@@ -79,13 +80,14 @@ def tile_attention_pb_t_kernel(tc, q_rot, k_rot, v, wo, out):
             )
 
         load_keys(0)
-        load_queries(0, 0)
+        load_queries(0, 0, range(REP))
+        load_queries(0, 0, range(REP, HEADS))
         load_values(0)
         nc.sync.dma_start(
             out=wo_sb[:].rearrange("p (a f) -> p a f", a=2), in_=wo.rearrange("(a p) f -> p a f", p=P)
         )
         for j in range(1, TILES):
-            load_queries(0, j)
+            load_queries(0, j, range(HEADS))
         out_flat = [out[b].rearrange("s k m -> (s k) m") for b in range(BATCH)]
 
         def out_rows(t, count):
@@ -216,8 +218,7 @@ def tile_attention_pb_t_kernel(tc, q_rot, k_rot, v, wo, out):
 
         def transpose_e(n, a):
             if a == 0:
-                eT_ps = eT_banks.tile([P, 2, WORDS, P], F32)
-                eT_of[n] = eT_ps
+                eT_of[n] = eT_banks.tile([P, 2, WORDS, P], F32, name="eT_ps", tag="eT")
             e_words = e_sb_of[n][:].bitcast(F32)
             for u in range(WORDS):
                 first = (WORDS * a + u) * P
@@ -246,17 +247,17 @@ def tile_attention_pb_t_kernel(tc, q_rot, k_rot, v, wo, out):
                 in_=e_grouped_of[r][:, heads.start : heads.stop, :, :].rearrange("p i q u -> p (i q u)").bitcast(BF16),
             )
 
-        def invert_sums(t, groups):
-            if groups.start == 0:
+        def invert_sums(t, heads):
+            if heads.start == 0:
                 inv_sum = per_tile.tile([P, HEADS], F32)
                 inv_sum_of[t] = inv_sum
-            some = slice(groups.start * REP, groups.stop * REP)
+            some = slice(heads.start, heads.stop)
             nc.vector.reciprocal(out=inv_sum_of[t][:, some], in_=row_sum_of[t][:, some])
 
-        def multiply_by_v(r, o_ps):
+        def multiply_by_v(r, o_ps, heads):
             b = r // (TILES * GROUPS)
             g_cols = slice((r % GROUPS) * HEAD_DIM, (r % GROUPS + 1) * HEAD_DIM)
-            for i in range(REP):
+            for i in heads:
                 q_cols = slice(i * P, (i + 1) * P)
                 nc.tensor.matmul_mx(
                     out=o_ps[:, i, :],
@@ -269,14 +270,20 @@ def tile_attention_pb_t_kernel(tc, q_rot, k_rot, v, wo, out):
                 )
             o_ps_of[r] = o_ps
 
-        def normalise(r):
+        def normalise(r, heads):
             t = r // GROUPS
             g = r % GROUPS
-            if g == 0:
+            if g == 0 and heads.start == 0:
                 o_sb = per_tile.tile([P, GROUPS, REP, HEAD_DIM], BF16)
                 o_sb_of[t] = o_sb
-            factors = inv_sum_of[t][:, g * REP : (g + 1) * REP].unsqueeze(2).to_broadcast([P, REP, HEAD_DIM])
-            nc.vector.tensor_tensor(out=o_sb_of[t][:, g, :, :], in0=o_ps_of[r][:], in1=factors, op=MULT)
+            some = slice(heads.start, heads.stop)
+            factors = inv_sum_of[t][:, g * REP + heads.start : g * REP + heads.stop]
+            nc.vector.tensor_tensor(
+                out=o_sb_of[t][:, g, some, :],
+                in0=o_ps_of[r][:, some, :],
+                in1=factors.unsqueeze(2).to_broadcast([P, len(heads), HEAD_DIM]),
+                op=MULT,
+            )
 
         def transpose_o(t, oT_ps, groups):
             for g in groups:
@@ -348,21 +355,23 @@ def tile_attention_pb_t_kernel(tc, q_rot, k_rot, v, wo, out):
 
         all_groups, all_heads = range(GROUPS), range(HEADS)
         unit_heads, round_heads = range(2), range(REP)
-        first_kT_ps = side_bank.tile([P, GROUPS, TILES, P], BF16, tag="side")
-        first_qT_ps = o_bank.tile([P, HEADS, P], BF16, tag="o")
-        transpose_keys(0, first_kT_ps, range(1))
-        keep_keys(0, first_kT_ps, range(1), nc.vector.tensor_copy)
-        transpose_queries(0, first_qT_ps, range(REP))
-        keep_queries(0, first_qT_ps, range(REP), nc.scalar.copy)
-        transpose_keys(0, first_kT_ps, range(1, GROUPS))
-        keep_keys(0, first_kT_ps, range(1, GROUPS), nc.vector.tensor_copy)
+        kT_ps = side_bank.tile([P, GROUPS, TILES, P], BF16, tag="side")
+        transpose_keys(0, kT_ps, range(1))
+        keep_keys(0, kT_ps, range(1), nc.vector.tensor_copy)
+        qT_ps = o_bank.tile([P, HEADS, P], BF16, tag="o")
+        transpose_queries(0, qT_ps, range(REP))
+        keep_queries(0, qT_ps, range(REP), nc.scalar.copy)
+        qT_ps = eT_banks.tile([P, HEADS, P], BF16, tag="eT")
+        transpose_queries(0, qT_ps, range(REP, HEADS))
+        keep_queries(0, qT_ps, range(REP, HEADS), nc.scalar.copy)
+        kT_ps = eT_banks.tile([P, GROUPS, TILES, P], BF16, tag="eT")
+        transpose_keys(0, kT_ps, range(1, GROUPS))
         for n in range(2):
             for a in range(2):
                 score_tile(n, a)
                 negate_maxima(n, a)
             if n == 0:
-                transpose_queries(0, first_qT_ps, range(REP, HEADS))
-                keep_queries(0, first_qT_ps, range(REP, HEADS), nc.scalar.copy)
+                keep_keys(0, kT_ps, range(1, GROUPS), nc.vector.tensor_copy)
 
         side_ps = None
         wo_ps = None
@@ -375,12 +384,14 @@ def tile_attention_pb_t_kernel(tc, q_rot, k_rot, v, wo, out):
                 if t % TILES == 0:
                     load_keys(t // TILES + 1)
                     load_values(t // TILES + 1)
-                load_queries(t // TILES + 1, t % TILES)
+                load_queries(t // TILES + 1, t % TILES, all_heads)
 
             if phase == 1 and 0 <= t - 2:
                 group_o(t - 2, side_ps, all_groups, nc.vector.tensor_copy)
             if phase == 0 and 0 <= t - 1:
-                invert_sums(t - 1, all_groups)
+                invert_sums(t - 1, all_heads)
+            if phase == 2 and new_batch:
+                keep_keys((t + 2) // TILES, side_ps, all_groups, nc.vector.tensor_copy)
             if phase == 2 and 0 <= t - 2:
                 quantise_o(t - 2, all_groups)
 
@@ -391,24 +402,20 @@ def tile_attention_pb_t_kernel(tc, q_rot, k_rot, v, wo, out):
                 transpose_e(n, a)
                 if n < UNITS_PER_TILE:
                     group_values(0, phase * 2 + a)
-
-            if n % 2 == 1 and t % TILES >= TILES // 2 and t // TILES + 1 < BATCH:
-                group_values(t // TILES + 1, n % VALUE_PIECES - 1)
-                group_values(t // TILES + 1, n % VALUE_PIECES)
+                elif n % 2 == 1 and t % TILES >= TILES // 2 and t // TILES + 1 < BATCH:
+                    group_values(t // TILES + 1, n % VALUE_PIECES - 1 + a)
 
             if 1 <= n:
                 group_e(n - 1, unit_heads, nc.scalar.copy)
             if (phase == 0 and 1 <= t or n == 1) and t + 1 < n_tiles:
                 keep_queries(t + 1, side_ps, all_heads, nc.scalar.copy)
-            if phase == 2 and new_batch:
-                keep_keys((t + 2) // TILES, side_ps, all_groups, nc.scalar.copy)
             if phase == 3 and 0 <= t - 2:
                 store(t - 2, side_ps, [nc.scalar.copy])
 
             if n % 2 == 1 and 5 <= n:
                 o_ps = o_bank.tile([P, REP, HEAD_DIM], F32, tag="o")
-                multiply_by_v((n - 5) // 2, o_ps)
-                normalise((n - 5) // 2)
+                multiply_by_v((n - 5) // 2, o_ps, round_heads)
+                normalise((n - 5) // 2, round_heads)
             if n % 2 == 0 and 2 <= n:
                 quantise_e((n - 2) // 2, round_heads)
             if phase == 0 and t % TILES == 0 and t > 0:
@@ -436,53 +443,58 @@ def tile_attention_pb_t_kernel(tc, q_rot, k_rot, v, wo, out):
                 transpose_queries(t + 2 if phase == 3 else 1, side_ps, all_heads)
 
         n, t, r = n_units - 1, n_tiles - 1, n_tiles * GROUPS - 1
+        first_pair, second_pair = range(REP // 2), range(REP // 2, REP)
 
-        def result_bank(r, bank, tag):
+        def result_in(bank, tag, r, heads):
             o_ps = bank.tile([P, REP, HEAD_DIM], F32, tag=tag)
-            multiply_by_v(r, o_ps)
+            multiply_by_v(r, o_ps, heads)
+
+        def turned_o_in(bank, tag, t, groups):
+            oT_ps = bank.tile([P, GROUPS, WORDS, P], F32, tag=tag)
+            transpose_o(t, oT_ps, groups)
+            return oT_ps
 
         exponential(n - 1, 0)
         transpose_e(n - 1, 0)
         exponential(n - 1, 1)
         transpose_e(n - 1, 1)
         group_e(n - 2, unit_heads, nc.scalar.copy)
-        result_bank(r - 2, o_bank, "o")
         quantise_o(t - 2, all_groups)
+        result_in(o_bank, "o", r - 2, round_heads)
         quantise_e(r - 1, round_heads)
-        normalise(r - 2)
-        invert_sums(t, range(1))
+        normalise(r - 2, round_heads)
+        invert_sums(t, range(REP))
 
         exponential(n, 0)
         transpose_e(n, 0)
-        side_ps = side_bank.tile([P, MODEL], F32, tag="side")
-        project(t - 2, side_ps, all_groups)
+        result_in(score_banks, "scores", r - 1, round_heads)
         exponential(n, 1)
         transpose_e(n, 1)
-        result_bank(r - 1, score_banks, "scores")
-        group_e(n - 1, unit_heads, nc.scalar.copy)
-        store(t - 2, side_ps, [nc.vector.tensor_copy])
-        normalise(r - 1)
-        group_e(n, unit_heads, nc.scalar.copy)
-        oT_ps = side_bank.tile([P, GROUPS, WORDS, P], F32, tag="side")
-        transpose_o(t - 1, oT_ps, all_groups)
-        group_o(t - 1, oT_ps, all_groups, nc.scalar.copy)
-        quantise_e(r, range(2))
-        invert_sums(t, range(1, GROUPS))
-        quantise_e(r, range(2, REP))
-        oT_ps = o_bank.tile([P, GROUPS, WORDS, P], F32, tag="o")
-        transpose_o(t, oT_ps, range(1))
-        result_bank(r, score_banks, "scores")
-        group_o(t, oT_ps, range(1), nc.scalar.copy)
-        quantise_o(t - 1, all_groups)
-        normalise(r)
-        out_ps = score_banks.tile([P, MODEL], F32, tag="scores")
-        project(t - 1, out_ps, all_groups)
-        store(t - 1, out_ps, [nc.scalar.copy])
-        quantise_o(t, range(1))
-        oT_ps = score_banks.tile([P, GROUPS, WORDS, P], F32, tag="scores")
-        transpose_o(t, oT_ps, range(1, GROUPS))
-        group_o(t, oT_ps, range(1, GROUPS), nc.vector.tensor_copy)
-        quantise_o(t, range(1, GROUPS))
+        turned_1 = turned_o_in(score_banks, "scores", t - 1, all_groups)
         side_ps = side_bank.tile([P, MODEL], F32, tag="side")
-        project(t, side_ps, all_groups)
-        store(t, side_ps, [nc.vector.tensor_copy, nc.scalar.copy])
+        project(t - 2, side_ps, all_groups)
+        group_e(n - 1, unit_heads, nc.scalar.copy)
+        group_e(n, unit_heads, nc.scalar.copy)
+        quantise_e(r, first_pair)
+        normalise(r - 1, round_heads)
+        invert_sums(t, range(REP, HEADS))
+        result_in(score_banks, "scores", r, first_pair)
+        turned_0 = turned_o_in(o_bank, "o", t, range(1))
+        quantise_e(r, second_pair)
+        group_o(t - 1, turned_1, all_groups, nc.scalar.copy)
+        normalise(r, first_pair)
+        result_in(score_banks, "scores", r, second_pair)
+        group_o(t, turned_0, range(1), nc.scalar.copy)
+        store(t - 2, side_ps, [nc.scalar.copy])
+        normalise(r, second_pair)
+        turned_0 = turned_o_in(eT_banks, "eT", t, range(1, GROUPS))
+        quantise_o(t - 1, all_groups)
+        quantise_o(t, range(1))
+        group_o(t, turned_0, range(1, GROUPS), nc.vector.tensor_copy)
+        side_ps = side_bank.tile([P, MODEL], F32, tag="side")
+        project(t - 1, side_ps, all_groups)
+        quantise_o(t, range(1, GROUPS))
+        out_ps = score_banks.tile([P, MODEL], F32, tag="scores")
+        project(t, out_ps, all_groups)
+        store(t - 1, side_ps, [nc.scalar.copy])
+        store(t, out_ps, [nc.vector.tensor_copy, nc.scalar.copy])

@@ -270,6 +270,19 @@ def tile_attention_pb_t_kernel(tc, q_rot, k_rot, v, wo, out):
                 )
             o_ps_of[r] = o_ps
 
+        def keep_clock_up(r, spare_ps):
+            g_cols = slice((r % GROUPS) * HEAD_DIM, (r % GROUPS + 1) * HEAD_DIM)
+            b = r // (TILES * GROUPS)
+            nc.tensor.matmul_mx(
+                out=spare_ps[:],
+                lhsT=v_codes_of[b][:, g_cols].bitcast(FP8X4),
+                lhsT_scale=v_scales_of[b][:, g_cols],
+                rhs=e_codes_of[r][:].bitcast(FP8X4),
+                rhs_scale=e_scales_of[r][:],
+                start=True,
+                stop=True,
+            )
+
         def normalise(r, heads):
             t = r // GROUPS
             g = r % GROUPS
@@ -418,6 +431,9 @@ def tile_attention_pb_t_kernel(tc, q_rot, k_rot, v, wo, out):
                 normalise((n - 5) // 2, round_heads)
             if n % 2 == 0 and 2 <= n:
                 quantise_e((n - 2) // 2, round_heads)
+            if n % 2 == 0 and 8 <= n:
+                spare_ps = o_bank.tile([P, REP * P], F32, tag="o")
+                keep_clock_up((n - 6) // 2, spare_ps)
             if phase == 0 and t % TILES == 0 and t > 0:
                 quantise_values(t // TILES)
             if n in (0, 2):
@@ -456,8 +472,11 @@ def tile_attention_pb_t_kernel(tc, q_rot, k_rot, v, wo, out):
 
         exponential(n - 1, 0)
         transpose_e(n - 1, 0)
+        spare_ps = score_banks.tile([P, REP * P], F32, tag="scores")
+        keep_clock_up(r - 3, spare_ps)
         exponential(n - 1, 1)
         transpose_e(n - 1, 1)
+        keep_clock_up(r - 3, spare_ps)
         group_e(n - 2, unit_heads, nc.scalar.copy)
         quantise_o(t - 2, all_groups)
         result_in(o_bank, "o", r - 2, round_heads)

@@ -403,8 +403,6 @@ def tile_attention_pb_t_kernel(tc, q_rot, k_rot, v, wo, out):
                 group_o(t - 2, side_ps, all_groups, nc.vector.tensor_copy)
             if phase == 0 and 0 <= t - 1:
                 invert_sums(t - 1, all_heads)
-            if phase == 2 and new_batch:
-                keep_keys((t + 2) // TILES, side_ps, all_groups, nc.vector.tensor_copy)
             if phase == 2 and 0 <= t - 2:
                 quantise_o(t - 2, all_groups)
 
@@ -422,6 +420,8 @@ def tile_attention_pb_t_kernel(tc, q_rot, k_rot, v, wo, out):
                 group_e(n - 1, unit_heads, nc.scalar.copy)
             if (phase == 0 and 1 <= t or n == 1) and t + 1 < n_tiles:
                 keep_queries(t + 1, side_ps, all_heads, nc.scalar.copy)
+            if phase == 2 and new_batch:
+                keep_keys((t + 2) // TILES, side_ps, all_groups, nc.scalar.copy)
             if phase == 3 and 0 <= t - 2:
                 store(t - 2, side_ps, [nc.scalar.copy])
 

@@ -28,6 +28,7 @@ SCALE = HEAD_DIM ** -0.5
 UNITS_PER_TILE = 4
 VALUE_PIECES = 8
 WARM_UP = 5
+PARK_ROWS = P * HEADS // MODEL
 WORDS = 2
 
 FLOPS = 2 * BATCH * HEADS * POSITIONS * POSITIONS * HEAD_DIM * 2 + 2 * BATCH * POSITIONS * FEATURES * MODEL
@@ -37,13 +38,15 @@ def tile_attention_pb_t_kernel(tc, q_rot, k_rot, v, wo, out):
     nc = tc.nc
     n_tiles = BATCH * TILES
     n_units = n_tiles * UNITS_PER_TILE
+    last_turned = n_tiles - 6
     with ExitStack() as ctx:
         ctx.enter_context(tc.manual_schedule())
         constants = ctx.enter_context(tc.tile_pool(name="constants", bufs=1))
         resident = ctx.enter_context(tc.tile_pool(name="resident", bufs=1))
         per_batch = ctx.enter_context(tc.tile_pool(name="per_batch", bufs=2))
         per_tile = ctx.enter_context(tc.tile_pool(name="per_tile", bufs=4))
-        per_unit = ctx.enter_context(tc.tile_pool(name="per_unit", bufs=5))
+        per_unit = ctx.enter_context(tc.tile_pool(name="per_unit", bufs=4))
+        per_round = ctx.enter_context(tc.tile_pool(name="per_round", bufs=8))
         results = ctx.enter_context(tc.tile_pool(name="results", bufs=8))
         score_banks = ctx.enter_context(tc.psum_pool(name="score_banks", bufs=4))
         eT_banks = ctx.enter_context(tc.psum_pool(name="eT_banks", bufs=2))
@@ -112,7 +115,7 @@ def tile_attention_pb_t_kernel(tc, q_rot, k_rot, v, wo, out):
 
         kT_of, v_grouped_of, v_codes_of, v_scales_of = {}, {}, {}, {}
         qT_of, o_grouped_of, o_codes_of, o_scales_of = {}, {}, {}, {}
-        row_sum_of, inv_sum_of, o_ps_of, o_sb_of = {}, {}, {}, {}
+        row_sum_of, inv_sum_of, factors_of, o_ps_of, o_sb_of = {}, {}, {}, {}, {}
         row_max_of, neg_max_of, scores_of, e_sb_of, eT_of, e_grouped_of, e_codes_of, e_scales_of = (
             {}, {}, {}, {}, {}, {}, {}, {},
         )
@@ -236,8 +239,8 @@ def tile_attention_pb_t_kernel(tc, q_rot, k_rot, v, wo, out):
 
         def quantise_e(r, heads):
             if heads.start == 0:
-                e_codes = per_unit.tile([P, REP * P], U32, align_bytes=64)
-                e_scales = per_unit.tile([P, REP * P], U8, align_bytes=64)
+                e_codes = per_round.tile([P, REP * P], U32, align_bytes=64)
+                e_scales = per_round.tile([P, REP * P], U8, align_bytes=64)
                 e_codes_of[r] = e_codes
                 e_scales_of[r] = e_scales
             cols = slice(heads.start * P, heads.stop * P)
@@ -253,6 +256,13 @@ def tile_attention_pb_t_kernel(tc, q_rot, k_rot, v, wo, out):
                 inv_sum_of[t] = inv_sum
             some = slice(heads.start, heads.stop)
             nc.vector.reciprocal(out=inv_sum_of[t][:, some], in_=row_sum_of[t][:, some])
+
+        def spread_factors(t):
+            park = out_rows(t, PARK_ROWS).rearrange("r m -> (r m)")
+            nc.sync.dma_start(out=park.rearrange("(q h) -> q h", h=HEADS), in_=inv_sum_of[t][:])
+            factors = per_tile.tile([P, P * HEADS], F32)
+            nc.sync.dma_start(out=factors[:], in_=park.partition_broadcast(P))
+            factors_of[t] = factors
 
         def multiply_by_v(r, o_ps, heads):
             b = r // (TILES * GROUPS)
@@ -270,17 +280,32 @@ def tile_attention_pb_t_kernel(tc, q_rot, k_rot, v, wo, out):
                 )
             o_ps_of[r] = o_ps
 
-        def keep_clock_up(r, spare_ps):
+        def multiply_turned(r, o_ps):
             g_cols = slice((r % GROUPS) * HEAD_DIM, (r % GROUPS + 1) * HEAD_DIM)
             b = r // (TILES * GROUPS)
             nc.tensor.matmul_mx(
-                out=spare_ps[:],
+                out=o_ps[:],
                 lhsT=v_codes_of[b][:, g_cols].bitcast(FP8X4),
                 lhsT_scale=v_scales_of[b][:, g_cols],
                 rhs=e_codes_of[r][:].bitcast(FP8X4),
                 rhs_scale=e_scales_of[r][:],
                 start=True,
                 stop=True,
+            )
+
+            o_ps_of[r] = o_ps
+
+        def normalise_turned(r):
+            t = r // GROUPS
+            g = r % GROUPS
+            if g == 0:
+                o_turned = per_tile.tile([P, GROUPS, P, PACK], BF16, align_bytes=64)
+                o_grouped_of[t] = o_turned
+            nc.vector.tensor_tensor(
+                out=o_grouped_of[t][:, g, :, :],
+                in0=o_ps_of[r][:].rearrange("d (i q) -> d q i", i=REP),
+                in1=factors_of[t][:].rearrange("d (q h) -> d q h", h=HEADS)[:, :, g * REP : (g + 1) * REP],
+                op=MULT,
             )
 
         def normalise(r, heads):
@@ -324,14 +349,17 @@ def tile_attention_pb_t_kernel(tc, q_rot, k_rot, v, wo, out):
                 in_=o_grouped_of[t][:, groups.start : groups.stop, :, :].rearrange("d g q u -> d (g q u)").bitcast(BF16),
             )
 
+        def turned(t):
+            return t % 2 == 0 and t <= last_turned
+
         def project(t, out_ps, groups):
             for g in groups:
                 nc.tensor.matmul_mx(
                     out=out_ps[:],
                     lhsT=o_codes_of[t][:, g * P : (g + 1) * P].bitcast(FP8X4),
                     lhsT_scale=o_scales_of[t][:, g * P : (g + 1) * P],
-                    rhs=wo_codes[:, g * MODEL : (g + 1) * MODEL].bitcast(FP8X4),
-                    rhs_scale=wo_scales[:, g * MODEL : (g + 1) * MODEL],
+                    rhs=wo_codes[turned(t)][:, g * MODEL : (g + 1) * MODEL].bitcast(FP8X4),
+                    rhs_scale=wo_scales[turned(t)][:, g * MODEL : (g + 1) * MODEL],
                     start=(g == 0),
                     stop=(g == GROUPS - 1),
                 )
@@ -343,27 +371,41 @@ def tile_attention_pb_t_kernel(tc, q_rot, k_rot, v, wo, out):
                 copy(out=out_sb[:, c * width : (c + 1) * width], in_=out_ps[:, c * width : (c + 1) * width])
             nc.sync.dma_start(out=out_rows(t, P), in_=out_sb[:])
 
-        wo_grouped = constants.tile([P, GROUPS, MODEL, WORDS], F32, align_bytes=64)
-        wo_codes = constants.tile([P, GROUPS * MODEL], U32, align_bytes=64)
-        wo_scales = constants.tile([P, GROUPS * MODEL], U8, align_bytes=64)
+        wo_grouped, wo_codes, wo_scales = {}, {}, {}
+        for way in (False, True):
+            wo_grouped[way] = constants.tile([P, GROUPS, MODEL, PACK], BF16, name="wo_grouped%d" % way, align_bytes=64)
+            wo_codes[way] = constants.tile([P, GROUPS * MODEL], U32, name="wo_codes%d" % way, align_bytes=64)
+            wo_scales[way] = constants.tile([P, GROUPS * MODEL], U8, name="wo_scales%d" % way, align_bytes=64)
 
-        def transpose_wo(g):
-            wo_ps = o_bank.tile([P, WORDS, 2, P], F32, tag="o")
-            wo_words = wo_sb[:].bitcast(F32)
-            for u in range(WORDS):
-                for a in range(2):
-                    first = (a * FEATURES + g * REP * HEAD_DIM) // 2 + u * P
-                    nc.tensor.transpose(wo_ps[:, u, a, :], wo_words[:, first : first + P], identity_f32[:])
+        def transpose_wo(way, g):
+            if way:
+                wo_ps = o_bank.tile([P, REP, 2, P], BF16, name="wo_ps_turned", tag="o")
+                for i in range(REP):
+                    for a in range(2):
+                        first = a * FEATURES + (g * REP + i) * HEAD_DIM
+                        nc.tensor.transpose(wo_ps[:, i, a, :], wo_sb[:, first : first + HEAD_DIM], identity_bf16[:])
+            else:
+                wo_ps = o_bank.tile([P, WORDS, 2, P], F32, name="wo_ps_words", tag="o")
+                wo_words = wo_sb[:].bitcast(F32)
+                for u in range(WORDS):
+                    for a in range(2):
+                        first = (a * FEATURES + g * REP * HEAD_DIM) // 2 + u * P
+                        nc.tensor.transpose(wo_ps[:, u, a, :], wo_words[:, first : first + P], identity_f32[:])
             return wo_ps
 
-        def group_wo(g, wo_ps):
-            nc.vector.tensor_copy(out=wo_grouped[:, g, :, :], in_=wo_ps[:].rearrange("d u a m -> d (a m) u"))
+        def group_wo(way, g, wo_ps):
+            grouped = wo_grouped[way][:, g, :, :].rearrange("d m i -> d (m i)")
+            if not way:
+                grouped = grouped.bitcast(F32)
+            nc.vector.tensor_copy(
+                out=grouped.rearrange("d (m i) -> d m i", m=MODEL), in_=wo_ps[:].rearrange("d i a m -> d (a m) i")
+            )
 
-        def quantise_wo():
+        def quantise_wo(way):
             nc.vector.quantize_mx(
-                out=wo_codes[:].bitcast(FP8X4),
-                scales=wo_scales[:],
-                in_=wo_grouped[:].rearrange("d g m u -> d (g m u)").bitcast(BF16),
+                out=wo_codes[way][:].bitcast(FP8X4),
+                scales=wo_scales[way][:],
+                in_=wo_grouped[way][:].rearrange("d g m i -> d (g m i)"),
             )
 
         all_groups, all_heads = range(GROUPS), range(HEADS)
@@ -388,10 +430,12 @@ def tile_attention_pb_t_kernel(tc, q_rot, k_rot, v, wo, out):
 
         side_ps = None
         wo_ps = None
+        hurry = (last_turned + 3) * UNITS_PER_TILE
         for n in range(n_units - 2):
             phase = n % UNITS_PER_TILE
             t = n // UNITS_PER_TILE
             new_batch = (t + 2) % TILES == 0 and t + 2 < n_tiles
+            ready = t - 4 if turned(t - 2) else t - 2
 
             if phase == 1 and t // TILES + 1 < BATCH:
                 if t % TILES == 0:
@@ -399,61 +443,86 @@ def tile_attention_pb_t_kernel(tc, q_rot, k_rot, v, wo, out):
                     load_values(t // TILES + 1)
                 load_queries(t // TILES + 1, t % TILES, all_heads)
 
-            if phase == 1 and 0 <= t - 2:
+            if phase == 1 and 0 <= t - 2 and not turned(t - 2):
                 group_o(t - 2, side_ps, all_groups, nc.vector.tensor_copy)
             if phase == 0 and 0 <= t - 1:
                 invert_sums(t - 1, all_heads)
-            if phase == 2 and 0 <= t - 2:
-                quantise_o(t - 2, all_groups)
+                if turned(t - 1):
+                    spread_factors(t - 1)
+            if phase == 2 and new_batch:
+                keep_keys((t + 2) // TILES, side_ps, all_groups, nc.vector.tensor_copy)
+            if phase == 2 and 0 <= ready:
+                quantise_o(ready, all_groups)
+            if n == hurry + 4:
+                quantise_o(last_turned, all_groups)
 
             for a in range(2):
                 exponential(n, a)
                 score_tile(n + 2, a)
+                if n % 2 == 1 and UNITS_PER_TILE <= n and t % TILES >= TILES // 2 and t // TILES + 1 < BATCH:
+                    group_values(t // TILES + 1, n % VALUE_PIECES - 1 + a)
                 negate_maxima(n + 2, a)
                 transpose_e(n, a)
+                if phase == 0 and a == 0 and 1 <= n:
+                    group_e(n - 1, unit_heads, nc.scalar.copy)
+                    quantise_e((n - 2) // 2, round_heads)
                 if n < UNITS_PER_TILE:
                     group_values(0, phase * 2 + a)
-                elif n % 2 == 1 and t % TILES >= TILES // 2 and t // TILES + 1 < BATCH:
-                    group_values(t // TILES + 1, n % VALUE_PIECES - 1 + a)
 
-            if 1 <= n:
+            if 1 <= n and phase != 0:
                 group_e(n - 1, unit_heads, nc.scalar.copy)
             if (phase == 0 and 1 <= t or n == 1) and t + 1 < n_tiles:
                 keep_queries(t + 1, side_ps, all_heads, nc.scalar.copy)
-            if phase == 2 and new_batch:
-                keep_keys((t + 2) // TILES, side_ps, all_groups, nc.scalar.copy)
-            if phase == 3 and 0 <= t - 2:
-                store(t - 2, side_ps, [nc.scalar.copy])
+            if phase == 3 and 0 <= ready:
+                store(ready, side_ps, [nc.scalar.copy])
+            if n == hurry + 6:
+                store(last_turned, side_ps, [nc.scalar.copy])
 
-            if n % 2 == 1 and 5 <= n:
+            if n % 2 == 1 and 5 <= n and not turned((n - 5) // UNITS_PER_TILE):
                 o_ps = o_bank.tile([P, REP, HEAD_DIM], F32, tag="o")
                 multiply_by_v((n - 5) // 2, o_ps, round_heads)
                 normalise((n - 5) // 2, round_heads)
-            if n % 2 == 0 and 2 <= n:
+            late = (n - 13) // 2 if n % 2 == 1 and n < hurry else -1
+            if n in (hurry, hurry + 2):
+                late = last_turned * GROUPS + (n - hurry) // 2
+            if 0 <= late and turned(late // GROUPS):
+                o_ps = o_bank.tile([P, REP * P], F32, tag="o")
+                multiply_turned(late, o_ps)
+                normalise_turned(late)
+            if phase == 2:
                 quantise_e((n - 2) // 2, round_heads)
-            if n % 2 == 0 and 8 <= n:
+            if n % 2 == 0 and 8 <= n and n not in (hurry, hurry + 2):
                 spare_ps = o_bank.tile([P, REP * P], F32, tag="o")
-                keep_clock_up((n - 6) // 2, spare_ps)
+                multiply_turned((n - 6) // 2, spare_ps)
             if phase == 0 and t % TILES == 0 and t > 0:
                 quantise_values(t // TILES)
             if n in (0, 2):
-                wo_ps = transpose_wo(n // 2)
+                wo_ps = transpose_wo(False, n // 2)
             if n in (1, 3):
-                group_wo(n // 2, wo_ps)
+                group_wo(False, n // 2, wo_ps)
             if n == 4:
                 quantise_values(0)
             if n == 6:
-                quantise_wo()
+                quantise_wo(False)
+            if n in (4, 6):
+                wo_ps = transpose_wo(True, n // 2 - 2)
+            if n in (5, 7):
+                group_wo(True, n // 2 - 2, wo_ps)
+            if n == 8:
+                quantise_wo(True)
 
-            if phase == 0 and 0 <= t - 2:
+            if phase == 0 and 0 <= t - 2 and not turned(t - 2):
                 side_ps = side_bank.tile([P, GROUPS, WORDS, P], F32, tag="side")
                 transpose_o(t - 2, side_ps, all_groups)
             if phase == 1 and new_batch:
                 side_ps = side_bank.tile([P, GROUPS, TILES, P], BF16, tag="side")
                 transpose_keys((t + 2) // TILES, side_ps, all_groups)
-            if phase == 2 and 0 <= t - 2:
+            if n == hurry + 5:
                 side_ps = side_bank.tile([P, MODEL], F32, tag="side")
-                project(t - 2, side_ps, all_groups)
+                project(last_turned, side_ps, all_groups)
+            if phase == 2 and 0 <= ready:
+                side_ps = side_bank.tile([P, MODEL], F32, tag="side")
+                project(ready, side_ps, all_groups)
             if phase == 3 and t + 2 < n_tiles or n == 0:
                 side_ps = side_bank.tile([P, HEADS, P], BF16, tag="side")
                 transpose_queries(t + 2 if phase == 3 else 1, side_ps, all_heads)
@@ -473,10 +542,10 @@ def tile_attention_pb_t_kernel(tc, q_rot, k_rot, v, wo, out):
         exponential(n - 1, 0)
         transpose_e(n - 1, 0)
         spare_ps = score_banks.tile([P, REP * P], F32, tag="scores")
-        keep_clock_up(r - 3, spare_ps)
+        multiply_turned(r - 3, spare_ps)
         exponential(n - 1, 1)
         transpose_e(n - 1, 1)
-        keep_clock_up(r - 3, spare_ps)
+        multiply_turned(r - 3, spare_ps)
         group_e(n - 2, unit_heads, nc.scalar.copy)
         quantise_o(t - 2, all_groups)
         result_in(o_bank, "o", r - 2, round_heads)

from contextlib import ExitStack

import concourse.mybir as mybir
from concourse.masks import make_identity

F32 = mybir.dt.float32
BF16 = mybir.dt.bfloat16
U32 = mybir.dt.uint32
U8 = mybir.dt.uint8
FP8X4 = mybir.dt.float8_e4m3fn_x4
EXP = mybir.ActivationFunctionType.Exp
ALONG_ROW = mybir.AxisListType.X
MULT = mybir.AluOpType.mult
ADD = mybir.AluOpType.add

P = 128
PACK = 4
BATCH = 8
POSITIONS = 512
TILES = POSITIONS // P
GROUPS = 2
REP = 4
HEADS = GROUPS * REP
HEAD_DIM = 128
FEATURES = HEADS * HEAD_DIM
MODEL = 256
SCALE = HEAD_DIM ** -0.5
UNITS_PER_TILE = 4
VALUE_PIECES = 8
WARM_UP = 5
PARK_ROWS = P * HEADS // MODEL
WORDS = 2

FLOPS = 2 * BATCH * HEADS * POSITIONS * POSITIONS * HEAD_DIM * 2 + 2 * BATCH * POSITIONS * FEATURES * MODEL


def tile_attention_pb_t_kernel(tc, q_rot, k_rot, v, wo, out):
    nc = tc.nc
    n_tiles = BATCH * TILES
    n_units = n_tiles * UNITS_PER_TILE
    last_turned = n_tiles - 6
    with ExitStack() as ctx:
        ctx.enter_context(tc.manual_schedule())
        constants = ctx.enter_context(tc.tile_pool(name="constants", bufs=1))
        resident = ctx.enter_context(tc.tile_pool(name="resident", bufs=1))
        per_batch = ctx.enter_context(tc.tile_pool(name="per_batch", bufs=2))
        per_tile = ctx.enter_context(tc.tile_pool(name="per_tile", bufs=4))
        per_unit = ctx.enter_context(tc.tile_pool(name="per_unit", bufs=4))
        per_round = ctx.enter_context(tc.tile_pool(name="per_round", bufs=8))
        results = ctx.enter_context(tc.tile_pool(name="results", bufs=8))
        score_banks = ctx.enter_context(tc.psum_pool(name="score_banks", bufs=4))
        eT_banks = ctx.enter_context(tc.psum_pool(name="eT_banks", bufs=2))
        o_bank = ctx.enter_context(tc.psum_pool(name="o_bank", bufs=1))
        side_bank = ctx.enter_context(tc.psum_pool(name="side_bank", bufs=1))

        k_sb, q_sb, v_sb = [], [], []
        for b in range(BATCH):
            keys = resident.tile([P, TILES, GROUPS * HEAD_DIM], BF16, name="keys%d" % b)
            queries = resident.tile([P, TILES, FEATURES], BF16, name="queries%d" % b)
            values = resident.tile([P, PACK, GROUPS * HEAD_DIM], BF16, name="values%d" % b)
            k_sb.append(keys)
            q_sb.append(queries)
            v_sb.append(values)
        wo_sb = resident.tile([P, 2 * FEATURES], BF16)

        def load_keys(b):
            nc.sync.dma_start(
                out=k_sb[b][:],
                in_=k_rot[b].rearrange("s k g d -> (s k) (g d)").rearrange("(t p) f -> p t f", p=P),
            )

        def load_queries(b, j, heads):
            cols = slice(heads.start * HEAD_DIM, heads.stop * HEAD_DIM)
            nc.sync.dma_start(
                out=q_sb[b][:, j, cols],
                in_=q_rot[b].rearrange("s k h d -> (s k) (h d)")[j * P : (j + 1) * P, cols],
            )

        def load_values(b):
            nc.sync.dma_start(
                out=v_sb[b][:].rearrange("p (u e) c -> p u (e c)", u=2),
                in_=v[b].rearrange("s k g d -> (s k) (g d)").rearrange("(u p e) c -> p u (e c)", u=2, e=2),
            )

        load_keys(0)
        load_queries(0, 0, range(REP))
        load_queries(0, 0, range(REP, HEADS))
        load_values(0)
        nc.sync.dma_start(
            out=wo_sb[:].rearrange("p (a f) -> p a f", a=2), in_=wo.rearrange("(a p) f -> p a f", p=P)
        )
        for j in range(1, TILES):
            load_queries(0, j, range(HEADS))
        out_flat = [out[b].rearrange("s k m -> (s k) m") for b in range(BATCH)]

        def out_rows(t, count):
            first = (t % TILES) * P
            return out_flat[t // TILES][first : first + count, :]

        identity_bf16 = constants.tile([P, P], BF16)
        make_identity(nc, identity_bf16[:])
        identity_f32 = constants.tile([P, P], F32)
        make_identity(nc, identity_f32[:])

        zero = constants.tile([P, 1], F32)
        nc.vector.memset(zero[:], 0.0)
        one = constants.tile([P, 1], F32)
        nc.scalar.activation(out=one[:], in_=zero[:], func=EXP)

        zeros = constants.tile([P, POSITIONS], BF16)
        nc.vector.memset(zeros[:], 0.0)
        warm_ps = score_banks.tile([P, POSITIONS], F32, tag="scores")
        for i in range(WARM_UP):
            nc.tensor.matmul(out=warm_ps[:], lhsT=zeros[:, :P], rhs=zeros[:], start=True, stop=True)

        kT_of, v_grouped_of, v_codes_of, v_scales_of = {}, {}, {}, {}
        qT_of, o_grouped_of, o_codes_of, o_scales_of = {}, {}, {}, {}
        row_sum_of, inv_sum_of, factors_of, o_ps_of, o_sb_of = {}, {}, {}, {}, {}
        row_max_of, neg_max_of, scores_of, e_sb_of, eT_of, e_grouped_of, e_codes_of, e_scales_of = (
            {}, {}, {}, {}, {}, {}, {}, {},
        )

        def transpose_keys(b, kT_ps, groups):
            for g in groups:
                for t in range(TILES):
                    nc.tensor.transpose(
                        kT_ps[:, g, t, :], k_sb[b][:, t, g * HEAD_DIM : (g + 1) * HEAD_DIM], identity_bf16[:]
                    )

        def keep_keys(b, kT_ps, groups, copy):
            if b not in kT_of:
                kT = per_batch.tile([P, GROUPS, POSITIONS], BF16)
                kT_of[b] = kT
            some = slice(groups.start, groups.stop)
            copy(
                out=kT_of[b][:, some, :].rearrange("d g k -> d (g k)").bitcast(F32),
                in_=kT_ps[:, some, :, :].rearrange("d g t k -> d (g t k)").bitcast(F32),
            )

        def transpose_queries(t, qT_ps, heads):
            for h in heads:
                nc.tensor.transpose(
                    qT_ps[:, h, :],
                    q_sb[t // TILES][:, t % TILES, h * HEAD_DIM : (h + 1) * HEAD_DIM],
                    identity_bf16[:],
                )

        def keep_queries(t, qT_ps, heads, copy):
            if t not in qT_of:
                qT = per_tile.tile([P, HEADS, P], BF16)
                qT_of[t] = qT
            some = slice(heads.start, heads.stop)
            copy(
                out=qT_of[t][:, some, :].rearrange("d h q -> d (h q)").bitcast(F32),
                in_=qT_ps[:, some, :].rearrange("d h q -> d (h q)").bitcast(F32),
            )

        def group_values(b, piece):
            if piece == 0:
                v_grouped = per_batch.tile([P, GROUPS * HEAD_DIM, PACK], BF16, align_bytes=64)
                v_grouped_of[b] = v_grouped
            width = GROUPS * HEAD_DIM // VALUE_PIECES
            cols = slice(piece * width, (piece + 1) * width)
            nc.gpsimd.tensor_scalar(
                out=v_grouped_of[b][:, cols, :],
                in0=v_sb[b][:, :, cols].rearrange("p t c -> p c t"),
                scalar1=1.0,
                scalar2=0.0,
                op0=MULT,
                op1=ADD,
            )

        def quantise_values(b):
            v_codes = per_batch.tile([P, GROUPS * HEAD_DIM], U32, align_bytes=64)
            v_scales = per_batch.tile([P, GROUPS * HEAD_DIM], U8, align_bytes=64)
            nc.vector.quantize_mx(
                out=v_codes[:].bitcast(FP8X4),
                scales=v_scales[:],
                in_=v_grouped_of[b][:].rearrange("p c t -> p (c t)"),
            )
            v_codes_of[b] = v_codes
            v_scales_of[b] = v_scales

        def score_tile(n, a):
            t = n // UNITS_PER_TILE
            head = (n % UNITS_PER_TILE) * 2 + a
            if a == 0:
                row_max = per_unit.tile([P, 2], F32)
                row_max_of[n] = row_max
            s_ps = score_banks.tile([P, POSITIONS], F32, tag="scores")
            nc.tensor.matmul(
                out=s_ps[:], lhsT=qT_of[t][:, head, :], rhs=kT_of[t // TILES][:, head // REP, :], start=True, stop=True
            )
            nc.vector.reduce_max(out=row_max_of[n][:, a : a + 1], in_=s_ps[:], axis=ALONG_ROW)
            scores_of[n, a] = s_ps

        def negate_maxima(n, a):
            if a == 0:
                neg_max = per_unit.tile([P, 2], F32)
                neg_max_of[n] = neg_max
            nc.gpsimd.tensor_scalar_mul(
                out=neg_max_of[n][:, a : a + 1], in0=row_max_of[n][:, a : a + 1], scalar1=-SCALE
            )

        def exponential(n, a):
            if a == 0:
                e_sb = per_unit.tile([P, 2 * POSITIONS], BF16)
                e_sb_of[n] = e_sb
                if n % UNITS_PER_TILE == 0:
                    row_sum = per_tile.tile([P, HEADS], F32)
                    row_sum_of[n // UNITS_PER_TILE] = row_sum
            head = (n % UNITS_PER_TILE) * 2 + a
            nc.scalar.activation(
                out=e_sb_of[n][:, a * POSITIONS : (a + 1) * POSITIONS],
                in_=scores_of[n, a][:],
                func=EXP,
                bias=neg_max_of[n][:, a : a + 1],
                scale=SCALE,
                accum_out=row_sum_of[n // UNITS_PER_TILE][:, head : head + 1],
            )

        def transpose_e(n, a):
            if a == 0:
                eT_of[n] = eT_banks.tile([P, 2, WORDS, P], F32, name="eT_ps", tag="eT")
            e_words = e_sb_of[n][:].bitcast(F32)
            for u in range(WORDS):
                first = (WORDS * a + u) * P
                nc.tensor.transpose(eT_of[n][:, a, u, :], e_words[:, first : first + P], identity_f32[:])

        def group_e(n, heads, copy):
            if n % 2 == 0 and heads.start == 0:
                e_grouped = per_unit.tile([P, REP, P, WORDS], F32, align_bytes=64)
                e_grouped_of[n // 2] = e_grouped
            first = (n % 2) * 2
            copy(
                out=e_grouped_of[n // 2][:, first + heads.start : first + heads.stop, :, :],
                in_=eT_of[n][:, heads.start : heads.stop, :, :].rearrange("p a u q -> p a q u"),
            )

        def quantise_e(r, heads):
            if heads.start == 0:
                e_codes = per_round.tile([P, REP * P], U32, align_bytes=64)
                e_scales = per_round.tile([P, REP * P], U8, align_bytes=64)
                e_codes_of[r] = e_codes
                e_scales_of[r] = e_scales
            cols = slice(heads.start * P, heads.stop * P)
            nc.vector.quantize_mx(
                out=e_codes_of[r][:, cols].bitcast(FP8X4),
                scales=e_scales_of[r][:, cols],
                in_=e_grouped_of[r][:, heads.start : heads.stop, :, :].rearrange("p i q u -> p (i q u)").bitcast(BF16),
            )

        def invert_sums(t, heads):
            if heads.start == 0:
                inv_sum = per_tile.tile([P, HEADS], F32)
                inv_sum_of[t] = inv_sum
            some = slice(heads.start, heads.stop)
            nc.vector.reciprocal(out=inv_sum_of[t][:, some], in_=row_sum_of[t][:, some])

        def spread_factors(t):
            park = out_rows(t, PARK_ROWS).rearrange("r m -> (r m)")
            nc.sync.dma_start(out=park.rearrange("(q h) -> q h", h=HEADS), in_=inv_sum_of[t][:])
            factors = per_tile.tile([P, P * HEADS], F32)
            nc.sync.dma_start(out=factors[:], in_=park.partition_broadcast(P))
            factors_of[t] = factors

        def multiply_by_v(r, o_ps, heads):
            b = r // (TILES * GROUPS)
            g_cols = slice((r % GROUPS) * HEAD_DIM, (r % GROUPS + 1) * HEAD_DIM)
            for i in heads:
                q_cols = slice(i * P, (i + 1) * P)
                nc.tensor.matmul_mx(
                    out=o_ps[:, i, :],
                    lhsT=e_codes_of[r][:, q_cols].bitcast(FP8X4),
                    lhsT_scale=e_scales_of[r][:, q_cols],
                    rhs=v_codes_of[b][:, g_cols].bitcast(FP8X4),
                    rhs_scale=v_scales_of[b][:, g_cols],
                    start=True,
                    stop=True,
                )
            o_ps_of[r] = o_ps

        def multiply_turned(r, o_ps):
            g_cols = slice((r % GROUPS) * HEAD_DIM, (r % GROUPS + 1) * HEAD_DIM)
            b = r // (TILES * GROUPS)
            nc.tensor.matmul_mx(
                out=o_ps[:],
                lhsT=v_codes_of[b][:, g_cols].bitcast(FP8X4),
                lhsT_scale=v_scales_of[b][:, g_cols],
                rhs=e_codes_of[r][:].bitcast(FP8X4),
                rhs_scale=e_scales_of[r][:],
                start=True,
                stop=True,
            )

            o_ps_of[r] = o_ps

        def normalise_turned(r):
            t = r // GROUPS
            g = r % GROUPS
            if g == 0:
                o_turned = per_tile.tile([P, GROUPS, P, PACK], BF16, align_bytes=64)
                o_grouped_of[t] = o_turned
            nc.vector.tensor_tensor(
                out=o_grouped_of[t][:, g, :, :],
                in0=o_ps_of[r][:].rearrange("d (i q) -> d q i", i=REP),
                in1=factors_of[t][:].rearrange("d (q h) -> d q h", h=HEADS)[:, :, g * REP : (g + 1) * REP],
                op=MULT,
            )

        def normalise(r, heads):
            t = r // GROUPS
            g = r % GROUPS
            if g == 0 and heads.start == 0:
                o_sb = per_tile.tile([P, GROUPS, REP, HEAD_DIM], BF16)
                o_sb_of[t] = o_sb
            some = slice(heads.start, heads.stop)
            factors = inv_sum_of[t][:, g * REP + heads.start : g * REP + heads.stop]
            nc.vector.tensor_tensor(
                out=o_sb_of[t][:, g, some, :],
                in0=o_ps_of[r][:, some, :],
                in1=factors.unsqueeze(2).to_broadcast([P, len(heads), HEAD_DIM]),
                op=MULT,
            )

        def transpose_o(t, oT_ps, groups):
            for g in groups:
                o_words = o_sb_of[t][:, g, :, :].rearrange("q i d -> q (i d)").bitcast(F32)
                for u in range(WORDS):
                    nc.tensor.transpose(oT_ps[:, g, u, :], o_words[:, u * P : (u + 1) * P], identity_f32[:])

        def group_o(t, oT_ps, groups, copy):
            if groups.start == 0:
                o_grouped = per_tile.tile([P, GROUPS, P, WORDS], F32, align_bytes=64)
                o_grouped_of[t] = o_grouped
            some = slice(groups.start, groups.stop)
            copy(out=o_grouped_of[t][:, some, :, :], in_=oT_ps[:, some, :, :].rearrange("d g u q -> d g q u"))

        def quantise_o(t, groups):
            if groups.start == 0:
                o_codes = per_tile.tile([P, GROUPS * P], U32, align_bytes=64)
                o_scales = per_tile.tile([P, GROUPS * P], U8, align_bytes=64)
                o_codes_of[t] = o_codes
                o_scales_of[t] = o_scales
            cols = slice(groups.start * P, groups.stop * P)
            nc.vector.quantize_mx(
                out=o_codes_of[t][:, cols].bitcast(FP8X4),
                scales=o_scales_of[t][:, cols],
                in_=o_grouped_of[t][:, groups.start : groups.stop, :, :].rearrange("d g q u -> d (g q u)").bitcast(BF16),
            )

        def turned(t):
            return t % 2 == 0 and t <= last_turned

        def project(t, out_ps, groups):
            for g in groups:
                nc.tensor.matmul_mx(
                    out=out_ps[:],
                    lhsT=o_codes_of[t][:, g * P : (g + 1) * P].bitcast(FP8X4),
                    lhsT_scale=o_scales_of[t][:, g * P : (g + 1) * P],
                    rhs=wo_codes[turned(t)][:, g * MODEL : (g + 1) * MODEL].bitcast(FP8X4),
                    rhs_scale=wo_scales[turned(t)][:, g * MODEL : (g + 1) * MODEL],
                    start=(g == 0),
                    stop=(g == GROUPS - 1),
                )

        def store(t, out_ps, copies):
            out_sb = results.tile([P, MODEL], F32)
            width = MODEL // len(copies)
            for c, copy in enumerate(copies):
                copy(out=out_sb[:, c * width : (c + 1) * width], in_=out_ps[:, c * width : (c + 1) * width])
            nc.sync.dma_start(out=out_rows(t, P), in_=out_sb[:])

        wo_grouped, wo_codes, wo_scales = {}, {}, {}
        for way in (False, True):
            wo_grouped[way] = constants.tile([P, GROUPS, MODEL, PACK], BF16, name="wo_grouped%d" % way, align_bytes=64)
            wo_codes[way] = constants.tile([P, GROUPS * MODEL], U32, name="wo_codes%d" % way, align_bytes=64)
            wo_scales[way] = constants.tile([P, GROUPS * MODEL], U8, name="wo_scales%d" % way, align_bytes=64)

        def transpose_wo(way, g):
            if way:
                wo_ps = o_bank.tile([P, REP, 2, P], BF16, name="wo_ps_turned", tag="o")
                for i in range(REP):
                    for a in range(2):
                        first = a * FEATURES + (g * REP + i) * HEAD_DIM
                        nc.tensor.transpose(wo_ps[:, i, a, :], wo_sb[:, first : first + HEAD_DIM], identity_bf16[:])
            else:
                wo_ps = o_bank.tile([P, WORDS, 2, P], F32, name="wo_ps_words", tag="o")
                wo_words = wo_sb[:].bitcast(F32)
                for u in range(WORDS):
                    for a in range(2):
                        first = (a * FEATURES + g * REP * HEAD_DIM) // 2 + u * P
                        nc.tensor.transpose(wo_ps[:, u, a, :], wo_words[:, first : first + P], identity_f32[:])
            return wo_ps

        def group_wo(way, g, wo_ps):
            grouped = wo_grouped[way][:, g, :, :].rearrange("d m i -> d (m i)")
            if not way:
                grouped = grouped.bitcast(F32)
            nc.vector.tensor_copy(
                out=grouped.rearrange("d (m i) -> d m i", m=MODEL), in_=wo_ps[:].rearrange("d i a m -> d (a m) i")
            )

        def quantise_wo(way):
            nc.vector.quantize_mx(
                out=wo_codes[way][:].bitcast(FP8X4),
                scales=wo_scales[way][:],
                in_=wo_grouped[way][:].rearrange("d g m i -> d (g m i)"),
            )

        all_groups, all_heads = range(GROUPS), range(HEADS)
        unit_heads, round_heads = range(2), range(REP)
        kT_ps = side_bank.tile([P, GROUPS, TILES, P], BF16, tag="side")
        transpose_keys(0, kT_ps, range(1))
        keep_keys(0, kT_ps, range(1), nc.vector.tensor_copy)
        qT_ps = o_bank.tile([P, HEADS, P], BF16, tag="o")
        transpose_queries(0, qT_ps, range(REP))
        keep_queries(0, qT_ps, range(REP), nc.scalar.copy)
        qT_ps = eT_banks.tile([P, HEADS, P], BF16, tag="eT")
        transpose_queries(0, qT_ps, range(REP, HEADS))
        keep_queries(0, qT_ps, range(REP, HEADS), nc.scalar.copy)
        kT_ps = eT_banks.tile([P, GROUPS, TILES, P], BF16, tag="eT")
        transpose_keys(0, kT_ps, range(1, GROUPS))
        for n in range(2):
            for a in range(2):
                score_tile(n, a)
                negate_maxima(n, a)
            if n == 0:
                keep_keys(0, kT_ps, range(1, GROUPS), nc.vector.tensor_copy)

        side_ps = None
        wo_ps = None
        hurry = (last_turned + 3) * UNITS_PER_TILE
        for n in range(n_units - 2):
            phase = n % UNITS_PER_TILE
            t = n // UNITS_PER_TILE
            new_batch = (t + 2) % TILES == 0 and t + 2 < n_tiles
            ready = t - 4 if turned(t - 2) else t - 2

            if phase == 1 and t // TILES + 1 < BATCH:
                if t % TILES == 0:
                    load_keys(t // TILES + 1)
                    load_values(t // TILES + 1)
                load_queries(t // TILES + 1, t % TILES, all_heads)

            if phase == 1 and 0 <= t - 2 and not turned(t - 2):
                group_o(t - 2, side_ps, all_groups, nc.vector.tensor_copy)
            if phase == 0 and 0 <= t - 1:
                invert_sums(t - 1, all_heads)
                if turned(t - 1):
                    spread_factors(t - 1)
            if phase == 2 and new_batch:
                keep_keys((t + 2) // TILES, side_ps, all_groups, nc.vector.tensor_copy)
            if phase == 2 and 0 <= ready:
                quantise_o(ready, all_groups)
            if n == hurry + 4:
                quantise_o(last_turned, all_groups)

            for a in range(2):
                exponential(n, a)
                score_tile(n + 2, a)
                if n % 2 == 1 and UNITS_PER_TILE <= n and t % TILES >= TILES // 2 and t // TILES + 1 < BATCH:
                    group_values(t // TILES + 1, n % VALUE_PIECES - 1 + a)
                negate_maxima(n + 2, a)
                transpose_e(n, a)
                if phase == 0 and a == 0 and 1 <= n:
                    group_e(n - 1, unit_heads, nc.scalar.copy)
                    quantise_e((n - 2) // 2, round_heads)
                if n < UNITS_PER_TILE:
                    group_values(0, phase * 2 + a)

            if 1 <= n and phase != 0:
                group_e(n - 1, unit_heads, nc.scalar.copy)
            if (phase == 0 and 1 <= t or n == 1) and t + 1 < n_tiles:
                keep_queries(t + 1, side_ps, all_heads, nc.scalar.copy)
            if phase == 3 and 0 <= ready:
                store(ready, side_ps, [nc.scalar.copy])
            if n == hurry + 6:
                store(last_turned, side_ps, [nc.scalar.copy])

            if n % 2 == 1 and 5 <= n and not turned((n - 5) // UNITS_PER_TILE):
                o_ps = o_bank.tile([P, REP, HEAD_DIM], F32, tag="o")
                multiply_by_v((n - 5) // 2, o_ps, round_heads)
                normalise((n - 5) // 2, round_heads)
            late = (n - 13) // 2 if n % 2 == 1 and n < hurry else -1
            if n in (hurry, hurry + 2):
                late = last_turned * GROUPS + (n - hurry) // 2
            if 0 <= late and turned(late // GROUPS):
                o_ps = o_bank.tile([P, REP * P], F32, tag="o")
                multiply_turned(late, o_ps)
                normalise_turned(late)
            if phase == 2:
                quantise_e((n - 2) // 2, round_heads)
            if n % 2 == 0 and 8 <= n and n not in (hurry, hurry + 2):
                spare_ps = o_bank.tile([P, REP * P], F32, tag="o")
                multiply_turned((n - 6) // 2, spare_ps)
            if phase == 0 and t % TILES == 0 and t > 0:
                quantise_values(t // TILES)
            if n in (0, 2):
                wo_ps = transpose_wo(False, n // 2)
            if n in (1, 3):
                group_wo(False, n // 2, wo_ps)
            if n == 4:
                quantise_values(0)
            if n == 6:
                quantise_wo(False)
            if n in (4, 6):
                wo_ps = transpose_wo(True, n // 2 - 2)
            if n in (5, 7):
                group_wo(True, n // 2 - 2, wo_ps)
            if n == 8:
                quantise_wo(True)

            if phase == 0 and 0 <= t - 2 and not turned(t - 2):
                side_ps = side_bank.tile([P, GROUPS, WORDS, P], F32, tag="side")
                transpose_o(t - 2, side_ps, all_groups)
            if phase == 1 and new_batch:
                side_ps = side_bank.tile([P, GROUPS, TILES, P], BF16, tag="side")
                transpose_keys((t + 2) // TILES, side_ps, all_groups)
            if n == hurry + 5:
                side_ps = side_bank.tile([P, MODEL], F32, tag="side")
                project(last_turned, side_ps, all_groups)
            if phase == 2 and 0 <= ready:
                side_ps = side_bank.tile([P, MODEL], F32, tag="side")
                project(ready, side_ps, all_groups)
            if phase == 3 and t + 2 < n_tiles or n == 0:
                side_ps = side_bank.tile([P, HEADS, P], BF16, tag="side")
                transpose_queries(t + 2 if phase == 3 else 1, side_ps, all_heads)

        n, t, r = n_units - 1, n_tiles - 1, n_tiles * GROUPS - 1
        first_pair, second_pair = range(REP // 2), range(REP // 2, REP)

        def result_in(bank, tag, r, heads):
            o_ps = bank.tile([P, REP, HEAD_DIM], F32, tag=tag)
            multiply_by_v(r, o_ps, heads)

        def turned_o_in(bank, tag, t, groups):
            oT_ps = bank.tile([P, GROUPS, WORDS, P], F32, tag=tag)
            transpose_o(t, oT_ps, groups)
            return oT_ps

        exponential(n - 1, 0)
        transpose_e(n - 1, 0)
        spare_ps = score_banks.tile([P, REP * P], F32, tag="scores")
        multiply_turned(r - 3, spare_ps)
        exponential(n - 1, 1)
        transpose_e(n - 1, 1)
        multiply_turned(r - 3, spare_ps)
        group_e(n - 2, unit_heads, nc.scalar.copy)
        quantise_o(t - 2, all_groups)
        result_in(o_bank, "o", r - 2, round_heads)
        quantise_e(r - 1, round_heads)
        normalise(r - 2, round_heads)
        invert_sums(t, range(REP))

        exponential(n, 0)
        transpose_e(n, 0)
        result_in(score_banks, "scores", r - 1, round_heads)
        exponential(n, 1)
        transpose_e(n, 1)
        turned_1 = turned_o_in(score_banks, "scores", t - 1, all_groups)
        side_ps = side_bank.tile([P, MODEL], F32, tag="side")
        project(t - 2, side_ps, all_groups)
        group_e(n - 1, unit_heads, nc.scalar.copy)
        group_e(n, unit_heads, nc.scalar.copy)
        quantise_e(r, first_pair)
        normalise(r - 1, round_heads)
        invert_sums(t, range(REP, HEADS))
        result_in(score_banks, "scores", r, first_pair)
        turned_0 = turned_o_in(o_bank, "o", t, range(1))
        quantise_e(r, second_pair)
        group_o(t - 1, turned_1, all_groups, nc.scalar.copy)
        normalise(r, first_pair)
        result_in(score_banks, "scores", r, second_pair)
        group_o(t, turned_0, range(1), nc.scalar.copy)
        store(t - 2, side_ps, [nc.scalar.copy])
        normalise(r, second_pair)
        turned_0 = turned_o_in(eT_banks, "eT", t, range(1, GROUPS))
        quantise_o(t - 1, all_groups)
        quantise_o(t, range(1))
        group_o(t, turned_0, range(1, GROUPS), nc.vector.tensor_copy)
        side_ps = side_bank.tile([P, MODEL], F32, tag="side")
        project(t - 1, side_ps, all_groups)
        quantise_o(t, range(1, GROUPS))
        out_ps = score_banks.tile([P, MODEL], F32, tag="scores")
        project(t, out_ps, all_groups)
        store(t - 1, side_ps, [nc.scalar.copy])
        store(t, out_ps, [nc.vector.tensor_copy, nc.scalar.copy])
